import numpy as np
import ml_dtypes


def mxq(x, axis, fmt="e4m3"):
    dtype, down = {"e4m3": (ml_dtypes.float8_e4m3fn, 7), "e5m2": (ml_dtypes.float8_e5m2, 14)}[fmt]
    v = np.moveaxis(np.asarray(x, np.float32).astype(ml_dtypes.bfloat16).astype(np.float64), axis, -1)
    blocks = v.reshape(v.shape[:-1] + (-1, 32))
    amax = np.abs(blocks).max(-1, keepdims=True)
    byte = np.maximum(np.where(amax > 0, np.frexp(amax)[1] - 1 + 127, 0) - down, 1)
    scale = np.exp2(byte - 127.0)
    codes = (blocks / scale).astype(np.float32).astype(dtype).astype(np.float64)
    return np.moveaxis((codes * scale).reshape(v.shape), -1, axis)


WIDE = False


def mx_kscale(k):
    if not WIDE:
        return np.ones(k)
    levels = np.array([10, -10, 5, -5, 0])
    a = np.random.permutation(np.resize(levels, k // 512 * 4)).reshape(k // 512, 4)
    idx = np.arange(k)
    return np.exp2(a[idx // 512, idx % 128 // 32])


BF16 = ml_dtypes.bfloat16


def bf(x):
    return np.asarray(x, np.float32).astype(BF16)


def f64(x):
    return np.asarray(x).astype(np.float64)


B, HD, NH, H, W, F = 2, 1024, 8, 16, 32, 2048
HEAD = HD // NH
P = H * W


def rms_in(x, w, eps=1e-8):
    std = np.std(x, axis=(-2, -1), keepdims=True, ddof=1)
    return x / (std + eps) * w[None, :, None, None]


def setup_inputs():
    n = np.random.standard_normal
    s = mx_kscale(HD)

    def stream():
        return n((B, NH, H, W, HEAD)) * 0.35 * (0.5 + np.random.random((B, NH, 1, 1, HEAD))) + 0.5 * n((B, NH, 1, 1, HEAD))

    return {"xx": bf(stream()), "xy": bf(stream()),
            "x": bf(n((B, HD, H, W)) * (0.5 + np.random.random((B, HD, 1, 1))) + 0.5 * n((B, HD, 1, 1))),
            "norm2_w": bf((1.0 + 0.1 * n(HD)) * s),
            "out_w": bf(n((HD, HD)) / np.sqrt(HD) / s[None, :]),
            "out_b": bf(0.1 * n(HD)),
            "gamma_att": bf(0.5 + 0.2 * n(HD))}


def reference(xx, xy, x, norm2_w, out_w, out_b, gamma_att):
    a = (f64(xx) + f64(xy)) * 0.5
    a = a.transpose(0, 1, 4, 2, 3).reshape(B, HD, H, W)
    a = rms_in(a, f64(norm2_w)).reshape(B, HD, P)
    a = (mxq(f64(out_w), 1, "e4m3") @ mxq(a, 1, "e4m3")) + f64(out_b)[None, :, None]
    return a.reshape(B, HD, H, W) * f64(gamma_att)[None, :, None, None] + f64(x)

@@ -1,0 +1,252 @@
+from contextlib import ExitStack
+
+import concourse.mybir as mybir
+from concourse.masks import make_identity
+
+FLOPS = 2 * 1024 * 1024 * 1024
+
+F32 = mybir.dt.float32
+BF16 = mybir.dt.bfloat16
+U32 = mybir.dt.uint32
+U8 = mybir.dt.uint8
+FP8X4 = mybir.dt.float8_e4m3fn_x4
+ACT = mybir.ActivationFunctionType
+ALU = mybir.AluOpType
+
+P = 128
+B = 2
+NPOS = 512
+MEAN_N = 32
+
+
+def tile_axialattentionblock_pb_kernel(tc, xx, xy, x, norm2_w, out_w, out_b, gamma_att, out):
+    nc = tc.nc
+    with ExitStack() as ctx:
+        const = ctx.enter_context(tc.tile_pool(name="const", bufs=1))
+        inp = ctx.enter_context(tc.tile_pool(name="inp", bufs=1))
+        keep = ctx.enter_context(tc.tile_pool(name="keep", bufs=1))
+        apool = ctx.enter_context(tc.tile_pool(name="apool", bufs=4))
+        gpool = ctx.enter_context(tc.tile_pool(name="gpool", bufs=2))
+        wpool = ctx.enter_context(tc.tile_pool(name="wpool", bufs=2))
+        small = ctx.enter_context(tc.tile_pool(name="small", bufs=4))
+        ps_a = ctx.enter_context(tc.psum_pool(name="ps_a", bufs=4))
+        ps_m = ctx.enter_context(tc.psum_pool(name="ps_m", bufs=1))
+        ps_w = ctx.enter_context(tc.psum_pool(name="ps_w", bufs=3))
+
+        w_bf = const.tile([P, 8], BF16, name="w_bf")
+        gam_bf = const.tile([P, 8], BF16, name="gam_bf")
+        ob_bf = const.tile([P, 8], BF16, name="ob_bf")
+        with nc.allow_non_contiguous_dma(reason="three vectors of 1024 values"):
+            nc.scalar.dma_start(out=w_bf[:], in_=norm2_w.rearrange("(n c) -> c n", c=P))
+            nc.scalar.dma_start(out=gam_bf[:], in_=gamma_att.rearrange("(p m) -> p m", m=8))
+            nc.scalar.dma_start(out=ob_bf[:], in_=out_b.rearrange("(p m) -> p m", m=8))
+
+        streams = {}
+
+        def load_a(b, g):
+            for src, nm in ((xx, "xx"), (xy, "xy")):
+                t = inp.tile([P, 4, NPOS], BF16, name="%s_%d%d" % (nm, b, g))
+                nc.sync.dma_start(
+                    out=t[:],
+                    in_=src[b, 4 * g:4 * g + 4].rearrange("n h (q r) c -> (h q) n (r c)", r=4),
+                )
+                streams[(nm, b, g)] = t
+
+        w_view = out_w.rearrange("(p m) j -> p m j", m=8)
+        w_sb = []
+
+        def load_w(mc):
+            t = inp.tile([P, 2, 1024], BF16, name="w_sb%d" % mc)
+            nc.sync.dma_start(out=t[:], in_=w_view[:, 2 * mc:2 * mc + 2, :])
+            w_sb.append(t)
+
+        x_sb = []
+
+        def load_x(b):
+            t = inp.tile([P, 8, NPOS], BF16, name="x_sb%d" % b)
+            nc.sync.dma_start(out=t[:], in_=x[b].rearrange("(p m) h w -> p m (h w)", m=8))
+            x_sb.append(t)
+
+        load_a(0, 0)
+        load_a(0, 1)
+        for mc in range(4):
+            load_w(mc)
+        load_a(1, 0)
+        load_a(1, 1)
+        load_x(0)
+        load_x(1)
+
+        one = const.tile([P, 1], F32, name="one")
+        nc.vector.memset(one[:], 1.0)
+        warm = const.tile([P, 1], F32, name="warm")
+        nc.scalar.activation(out=warm[:], in_=one[:], func=ACT.Sqrt)
+        negc = const.tile([P, MEAN_N], BF16, name="negc")
+        nc.vector.memset(negc[:], -1.0 / NPOS)
+        ident_f = const.tile([P, P], F32, name="ident_f")
+        make_identity(nc, ident_f[:])
+        ident_b = const.tile([P, P], BF16, name="ident_b")
+        make_identity(nc, ident_b[:])
+
+        gam = const.tile([P, 8], F32, name="gam")
+        nc.vector.tensor_copy(out=gam[:], in_=gam_bf[:])
+        gb = const.tile([P, 8], F32, name="gb")
+        nc.vector.tensor_tensor(out=gb[:], in0=gam_bf[:], in1=ob_bf[:], op=ALU.mult)
+        w05 = const.tile([P, 8], F32, name="w05")
+        nc.vector.tensor_scalar(out=w05[:], in0=w_bf[:], scalar1=0.5, scalar2=None, op0=ALU.mult)
+
+        state = {}
+
+        def front(b, g):
+            xxt = streams[("xx", b, g)]
+            xyt = streams[("xy", b, g)]
+            mean_ps = ps_m.tile([P, 4, MEAN_N], F32, name="mean_ps")
+            for j in range(4):
+                k = 0
+                for src in (xxt, xyt):
+                    for r in range(4):
+                        nc.tensor.matmul(
+                            mean_ps[:, j, :],
+                            lhsT=src[:, j, P * r:P * r + P],
+                            rhs=negc[:],
+                            start=(k == 0),
+                            stop=(k == 7),
+                        )
+                        k += 1
+            negm = small.tile([P, 4], F32, name="negm")
+            nc.vector.tensor_copy(out=negm[:], in_=mean_ps[:, :, 0])
+            ssq = small.tile([P, 4], F32, name="ssq")
+            ats = []
+            for h in range(2):
+                a_sb = apool.tile([P, 2, NPOS], F32, name="a_sb")
+                nc.vector.tensor_tensor(
+                    out=a_sb[:], in0=xxt[:, 2 * h:2 * h + 2, :], in1=xyt[:, 2 * h:2 * h + 2, :], op=ALU.add
+                )
+                for i in range(2):
+                    at = ps_a.tile([P, NPOS], F32, name="at")
+                    for r in range(4):
+                        nc.tensor.transpose(at[:, P * r:P * r + P], a_sb[:, i, P * r:P * r + P], ident_f[:])
+                    ats.append(at)
+            for j in range(4):
+                junk = small.tile([P, NPOS], BF16, name="junk")
+                nc.scalar.activation(
+                    out=junk[:], in_=ats[j][:], func=ACT.Square,
+                    bias=negm[:, j:j + 1], scale=1.0, accum_out=ssq[:, j:j + 1],
+                )
+            state[(b, g)] = (ats, ssq)
+
+        gq = {}
+        gs = {}
+
+        def back(b, g):
+            ats, ssq = state[(b, g)]
+            std = small.tile([P, 4], F32, name="std")
+            nc.scalar.activation(out=std[:], in_=ssq[:], func=ACT.Sqrt, scale=1.0 / (4.0 * (NPOS - 1)))
+            den = small.tile([P, 4], F32, name="den")
+            nc.vector.tensor_scalar(out=den[:], in0=std[:], scalar1=1e-8, scalar2=None, op0=ALU.add)
+            rec = small.tile([P, 4], F32, name="rec")
+            nc.vector.reciprocal(out=rec[:], in_=den[:])
+            sc = small.tile([P, 4], F32, name="sc")
+            nc.vector.tensor_tensor(out=sc[:], in0=rec[:], in1=w05[:, 4 * g:4 * g + 4], op=ALU.mult)
+            g_t = gpool.tile([P, 4, NPOS], BF16, name="g_t")
+            for j in range(4):
+                nc.scalar.activation(
+                    out=g_t[:, j, :].rearrange("c (p r) -> c p r", r=4),
+                    in_=ats[j][:].rearrange("c (r p) -> c p r", r=4),
+                    func=ACT.Copy, scale=sc[:, j:j + 1],
+                )
+            grp = gpool.tile([P, NPOS, 4], BF16, name="grp", align_bytes=64)
+            nc.vector.tensor_copy(
+                out=grp[:].rearrange("p (c i) t -> p c t i", i=4),
+                in_=g_t[:].rearrange("p t (c i) -> p c t i", i=4),
+            )
+            codes = keep.tile([P, NPOS], U32, name="gq%d%d" % (b, g), align_bytes=64)
+            planes = keep.tile([P, NPOS], U8, name="gs%d%d" % (b, g), align_bytes=64)
+            nc.vector.quantize_mx(
+                out=codes[:].bitcast(FP8X4), scales=planes[:], in_=grp[:].rearrange("p w t -> p (w t)")
+            )
+            gq[(b, g)] = codes
+            gs[(b, g)] = planes
+
+        wq = []
+        ws = []
+
+        def wprep(mc):
+            wg = wpool.tile([P, 2, 2, P, 4], BF16, name="wg", align_bytes=64)
+            for i in range(2):
+                wt = ps_w.tile([P, 2, 4, P], BF16, name="wt", tag="wacc")
+                for g in range(2):
+                    for t in range(4):
+                        c0 = 512 * g + P * t
+                        nc.tensor.transpose(wt[:, g, t, :], w_sb[mc][:, i, c0:c0 + P], ident_b[:])
+                src = wt[:].rearrange("p g t o -> p g o t")
+                if i == 0:
+                    nc.vector.tensor_copy(out=wg[:, i], in_=src)
+                else:
+                    nc.scalar.copy(out=wg[:, i], in_=src)
+            codes = keep.tile([P, 4, P], U32, name="wq%d" % mc, align_bytes=64)
+            planes = keep.tile([P, 4, P], U8, name="ws%d" % mc, align_bytes=64)
+            nc.vector.quantize_mx(
+                out=codes[:].rearrange("p a o -> p (a o)").bitcast(FP8X4),
+                scales=planes[:].rearrange("p a o -> p (a o)"),
+                in_=wg[:].rearrange("p i g o t -> p (i g o t)"),
+            )
+            wq.append(codes)
+            ws.append(planes)
+
+        xp = {}
+
+        def xprep(b, mc):
+            t = keep.tile([P, 2, NPOS], F32, name="xp%d%d" % (b, mc))
+            for i in range(2):
+                m = 2 * mc + i
+                nc.gpsimd.tensor_scalar(
+                    out=t[:, i, :], in0=x_sb[b][:, m, :], scalar1=1.0, scalar2=gb[:, m:m + 1],
+                    op0=ALU.mult, op1=ALU.add,
+                )
+            xp[(b, mc)] = t
+
+        def outp(b, mc):
+            t = xp[(b, mc)]
+            for i in range(2):
+                m = 2 * mc + i
+                acc = ps_w.tile([P, NPOS], F32, name="acc", tag="wacc")
+                for g in range(2):
+                    nc.tensor.matmul_mx(
+                        out=acc[:],
+                        lhsT=wq[mc][:, 2 * i + g, :].bitcast(FP8X4),
+                        lhsT_scale=ws[mc][:, 2 * i + g, :],
+                        rhs=gq[(b, g)][:].bitcast(FP8X4),
+                        rhs_scale=gs[(b, g)][:],
+                        start=(g == 0),
+                        stop=(g == 1),
+                    )
+                nc.vector.scalar_tensor_tensor(
+                    out=t[:, i, :], in0=acc[:], scalar=gam[:, m:m + 1], in1=t[:, i, :],
+                    op0=ALU.mult, op1=ALU.add,
+                )
+            nc.sync.dma_start(
+                out=out[b].rearrange("(p m) h w -> p m (h w)", m=8)[:, 2 * mc:2 * mc + 2, :], in_=t[:]
+            )
+
+        front(0, 0)
+        back(0, 0)
+        front(0, 1)
+        wprep(0)
+        back(0, 1)
+        wprep(1)
+        wprep(2)
+        wprep(3)
+        front(1, 0)
+        for mc in range(4):
+            xprep(0, mc)
+        outp(0, 0)
+        outp(0, 1)
+        back(1, 0)
+        front(1, 1)
+        outp(0, 2)
+        outp(0, 3)
+        for mc in range(4):
+            xprep(1, mc)
+        back(1, 1)
+        for mc in range(4):
+            outp(1, mc)

@@ -14,9 +14,206 @@ ACT = mybir.ActivationFunctionType
 ALU = mybir.AluOpType
 
 P = 128
-B = 2
 NPOS = 512
-MEAN_N = 32
+MEAN_N = 2
+PINNED = True
+PE_ADD = (0, 1, 4)
+W_ON_V = (1, 4, 7)
+E_ON_V = ()
+X_ENGINE = ('V', 'S')
+A_BUFS = 5
+AT_BUFS = 4
+WACC_BUFS = 3
+PLAN = (
+    ('load_vec',),
+    ('consts',),
+    ('load_a', 0, True),
+    ('load_a', 1, False),
+    ('load_a', 2, False),
+    ('load_a', 3, False),
+    ('load_w', 0),
+    ('load_w', 1),
+    ('load_a', 4, False),
+    ('load_w', 2),
+    ('load_a', 5, False),
+    ('load_w', 3),
+    ('load_a', 6, False),
+    ('load_x', 0),
+    ('load_a', 7, False),
+    ('load_x', 1),
+    ('tr', 0, 0),
+    ('means', 0),
+    ('negmean', 0),
+    ('tr', 0, 1),
+    ('means', 1),
+    ('sq', 0, 0),
+    ('negmean', 1),
+    ('tr', 1, 0),
+    ('vec_w',),
+    ('sq', 0, 1),
+    ('root', 0),
+    ('chain', 0),
+    ('sq', 1, 0),
+    ('tr', 1, 1),
+    ('sq', 1, 1),
+    ('means', 2),
+    ('root', 1),
+    ('add', 2),
+    ('negmean', 2),
+    ('means', 3),
+    ('ev', 0, 0),
+    ('tr', 2, 0),
+    ('chain', 1),
+    ('ev', 1, 0),
+    ('ev', 0, 1),
+    ('ev', 1, 1),
+    ('sq', 2, 0),
+    ('wtr', 1),
+    ('tr', 2, 1),
+    ('sq', 2, 1),
+    ('negmean', 3),
+    ('wtr', 0),
+    ('add', 3),
+    ('regroup', 0),
+    ('root', 2),
+    ('chain', 2),
+    ('means', 4),
+    ('quant', 0),
+    ('wev', 1),
+    ('wev', 0),
+    ('ev', 2, 0),
+    ('wtr', 3),
+    ('tr', 3, 0),
+    ('tr', 3, 1),
+    ('sq', 3, 0),
+    ('wtr', 4),
+    ('negmean', 4),
+    ('means', 5),
+    ('wev', 3),
+    ('ev', 2, 1),
+    ('sq', 3, 1),
+    ('wquant', 0),
+    ('vec_g',),
+    ('wev', 4),
+    ('tr', 4, 0),
+    ('sq', 4, 0),
+    ('negmean', 5),
+    ('wtr', 2),
+    ('root', 3),
+    ('add', 5),
+    ('chain', 3),
+    ('tr', 4, 1),
+    ('sq', 4, 1),
+    ('root', 4),
+    ('wtr', 7),
+    ('wev', 2),
+    ('add', 6),
+    ('wtr', 5),
+    ('means', 6),
+    ('negmean', 6),
+    ('chain', 4),
+    ('ev', 3, 0),
+    ('ev', 4, 0),
+    ('ev', 3, 1),
+    ('wquant', 1),
+    ('ev', 4, 1),
+    ('wev', 7),
+    ('tr', 6, 0),
+    ('sq', 6, 0),
+    ('tr', 5, 1),
+    ('xprep', 0, 1),
+    ('tr', 5, 0),
+    ('sq', 5, 0),
+    ('means', 7),
+    ('sq', 5, 1),
+    ('xprep', 0, 0),
+    ('root', 5),
+    ('wev', 5),
+    ('regroup', 1),
+    ('tr', 6, 1),
+    ('quant', 1),
+    ('mx', 0, 0),
+    ('xprep', 0, 3),
+    ('add', 7),
+    ('xprep', 0, 6),
+    ('sq', 6, 1),
+    ('fin', 0, 0),
+    ('wquant', 2),
+    ('root', 6),
+    ('wtr', 6),
+    ('mx', 0, 1),
+    ('wev', 6),
+    ('chain', 6),
+    ('xprep', 0, 4),
+    ('ev', 6, 0),
+    ('mx', 0, 2),
+    ('fin', 0, 1),
+    ('wquant', 3),
+    ('chain', 5),
+    ('ev', 6, 1),
+    ('mx', 0, 3),
+    ('fin', 0, 3),
+    ('negmean', 7),
+    ('ev', 5, 0),
+    ('xprep', 0, 2),
+    ('fin', 0, 2),
+    ('xprep', 0, 5),
+    ('ev', 5, 1),
+    ('regroup', 2),
+    ('tr', 7, 0),
+    ('sq', 7, 0),
+    ('mx', 0, 6),
+    ('tr', 7, 1),
+    ('sq', 7, 1),
+    ('root', 7),
+    ('quant', 2),
+    ('chain', 7),
+    ('mx', 0, 4),
+    ('ev', 7, 1),
+    ('mx', 0, 5),
+    ('fin', 0, 4),
+    ('store', 0, 2, 2),
+    ('fin', 0, 6),
+    ('mx', 0, 7),
+    ('fin', 0, 5),
+    ('ev', 7, 0),
+    ('regroup', 3),
+    ('quant', 3),
+    ('mx', 1, 0),
+    ('xprep', 1, 0),
+    ('xprep', 1, 1),
+    ('xprep', 0, 7),
+    ('xprep', 1, 5),
+    ('xprep', 1, 6),
+    ('fin', 0, 7),
+    ('xprep', 1, 4),
+    ('fin', 1, 0),
+    ('mx', 1, 1),
+    ('store', 0, 4, 2),
+    ('mx', 1, 2),
+    ('store', 0, 0, 2),
+    ('mx', 1, 3),
+    ('fin', 1, 1),
+    ('mx', 1, 4),
+    ('store', 0, 6, 2),
+    ('store', 1, 1, 1),
+    ('xprep', 1, 2),
+    ('fin', 1, 2),
+    ('store', 1, 0, 1),
+    ('xprep', 1, 3),
+    ('fin', 1, 3),
+    ('store', 1, 2, 2),
+    ('fin', 1, 4),
+    ('mx', 1, 5),
+    ('fin', 1, 5),
+    ('mx', 1, 6),
+    ('mx', 1, 7),
+    ('xprep', 1, 7),
+    ('fin', 1, 6),
+    ('store', 1, 4, 2),
+    ('fin', 1, 7),
+    ('store', 1, 6, 2),
+)
 
 
 def tile_axialattentionblock_pb_kernel(tc, xx, xy, x, norm2_w, out_w, out_b, gamma_att, out):
@@ -25,228 +222,239 @@ def tile_axialattentionblock_pb_kernel(tc, xx, xy, x, norm2_w, out_w, out_b, gam
         const = ctx.enter_context(tc.tile_pool(name="const", bufs=1))
         inp = ctx.enter_context(tc.tile_pool(name="inp", bufs=1))
         keep = ctx.enter_context(tc.tile_pool(name="keep", bufs=1))
-        apool = ctx.enter_context(tc.tile_pool(name="apool", bufs=4))
+        apool = ctx.enter_context(tc.tile_pool(name="apool", bufs=A_BUFS))
         gpool = ctx.enter_context(tc.tile_pool(name="gpool", bufs=2))
         wpool = ctx.enter_context(tc.tile_pool(name="wpool", bufs=2))
         small = ctx.enter_context(tc.tile_pool(name="small", bufs=4))
-        ps_a = ctx.enter_context(tc.psum_pool(name="ps_a", bufs=4))
+        ps_a = ctx.enter_context(tc.psum_pool(name="ps_a", bufs=AT_BUFS))
         ps_m = ctx.enter_context(tc.psum_pool(name="ps_m", bufs=1))
-        ps_w = ctx.enter_context(tc.psum_pool(name="ps_w", bufs=3))
+        ps_w = ctx.enter_context(tc.psum_pool(name="ps_w", bufs=WACC_BUFS))
+        if PINNED:
+            ctx.enter_context(tc.manual_schedule())
 
         w_bf = const.tile([P, 8], BF16, name="w_bf")
         gam_bf = const.tile([P, 8], BF16, name="gam_bf")
         ob_bf = const.tile([P, 8], BF16, name="ob_bf")
-        with nc.allow_non_contiguous_dma(reason="three vectors of 1024 values"):
-            nc.scalar.dma_start(out=w_bf[:], in_=norm2_w.rearrange("(n c) -> c n", c=P))
-            nc.scalar.dma_start(out=gam_bf[:], in_=gamma_att.rearrange("(p m) -> p m", m=8))
-            nc.scalar.dma_start(out=ob_bf[:], in_=out_b.rearrange("(p m) -> p m", m=8))
-
-        streams = {}
-
-        def load_a(b, g):
-            for src, nm in ((xx, "xx"), (xy, "xy")):
-                t = inp.tile([P, 4, NPOS], BF16, name="%s_%d%d" % (nm, b, g))
-                nc.sync.dma_start(
-                    out=t[:],
-                    in_=src[b, 4 * g:4 * g + 4].rearrange("n h (q r) c -> (h q) n (r c)", r=4),
-                )
-                streams[(nm, b, g)] = t
-
+        one = const.tile([P, 1], F32, name="one")
+        warm = const.tile([P, 1], F32, name="warm")
+        negc = const.tile([P, MEAN_N], BF16, name="negc")
+        ident_f = const.tile([P, P], F32, name="ident_f")
+        ident_b = const.tile([P, P], BF16, name="ident_b")
+        gam = const.tile([P, 8], F32, name="gam")
+        gb = const.tile([P, 8], F32, name="gb")
+        w05 = const.tile([P, 8], F32, name="w05")
         w_view = out_w.rearrange("(p m) j -> p m j", m=8)
-        w_sb = []
+        st = {}
+
+        def load_vec():
+            with nc.allow_non_contiguous_dma(reason="three vectors of 1024 values"):
+                nc.scalar.dma_start(out=w_bf[:], in_=norm2_w.rearrange("(n c) -> c n", c=P))
+                nc.scalar.dma_start(out=gam_bf[:], in_=gamma_att.rearrange("(p m) -> p m", m=8))
+                nc.scalar.dma_start(out=ob_bf[:], in_=out_b.rearrange("(p m) -> p m", m=8))
+
+        def load_a(k, split):
+            b, n0 = k // 4, 2 * (k % 4)
+            tiles = []
+            for nm in ("xx", "xy"):
+                t = inp.tile([P, 2, NPOS], BF16, name="%s_%d" % (nm, k))
+                st[(nm, k)] = t
+                tiles.append(t)
+            if split:
+                for j in range(2):
+                    for src, t in zip((xx, xy), tiles):
+                        nc.sync.dma_start(
+                            out=t[:, j, :], in_=src[b, n0 + j].rearrange("h (q r) c -> (h q) (r c)", r=4))
+            else:
+                for src, t in zip((xx, xy), tiles):
+                    nc.sync.dma_start(
+                        out=t[:], in_=src[b, n0:n0 + 2].rearrange("n h (q r) c -> (h q) n (r c)", r=4))
 
         def load_w(mc):
             t = inp.tile([P, 2, 1024], BF16, name="w_sb%d" % mc)
             nc.sync.dma_start(out=t[:], in_=w_view[:, 2 * mc:2 * mc + 2, :])
-            w_sb.append(t)
-
-        x_sb = []
+            st[("w", mc)] = t
 
         def load_x(b):
             t = inp.tile([P, 8, NPOS], BF16, name="x_sb%d" % b)
             nc.sync.dma_start(out=t[:], in_=x[b].rearrange("(p m) h w -> p m (h w)", m=8))
-            x_sb.append(t)
+            st[("x", b)] = t
 
-        load_a(0, 0)
-        load_a(0, 1)
-        for mc in range(4):
-            load_w(mc)
-        load_a(1, 0)
-        load_a(1, 1)
-        load_x(0)
-        load_x(1)
+        def consts():
+            nc.vector.memset(one[:], 1.0)
+            nc.scalar.activation(out=warm[:], in_=one[:], func=ACT.Sqrt)
+            nc.vector.memset(negc[:], -1.0 / NPOS)
+            make_identity(nc, ident_b[:])
+            make_identity(nc, ident_f[:])
 
-        one = const.tile([P, 1], F32, name="one")
-        nc.vector.memset(one[:], 1.0)
-        warm = const.tile([P, 1], F32, name="warm")
-        nc.scalar.activation(out=warm[:], in_=one[:], func=ACT.Sqrt)
-        negc = const.tile([P, MEAN_N], BF16, name="negc")
-        nc.vector.memset(negc[:], -1.0 / NPOS)
-        ident_f = const.tile([P, P], F32, name="ident_f")
-        make_identity(nc, ident_f[:])
-        ident_b = const.tile([P, P], BF16, name="ident_b")
-        make_identity(nc, ident_b[:])
+        def vec_w():
+            nc.vector.tensor_scalar(out=w05[:], in0=w_bf[:], scalar1=0.5, scalar2=None, op0=ALU.mult)
 
-        gam = const.tile([P, 8], F32, name="gam")
-        nc.vector.tensor_copy(out=gam[:], in_=gam_bf[:])
-        gb = const.tile([P, 8], F32, name="gb")
-        nc.vector.tensor_tensor(out=gb[:], in0=gam_bf[:], in1=ob_bf[:], op=ALU.mult)
-        w05 = const.tile([P, 8], F32, name="w05")
-        nc.vector.tensor_scalar(out=w05[:], in0=w_bf[:], scalar1=0.5, scalar2=None, op0=ALU.mult)
+        def vec_g():
+            nc.vector.tensor_copy(out=gam[:], in_=gam_bf[:])
+            nc.vector.tensor_tensor(out=gb[:], in0=gam_bf[:], in1=ob_bf[:], op=ALU.mult)
 
-        state = {}
-
-        def front(b, g):
-            xxt = streams[("xx", b, g)]
-            xyt = streams[("xy", b, g)]
-            mean_ps = ps_m.tile([P, 4, MEAN_N], F32, name="mean_ps")
-            for j in range(4):
-                k = 0
-                for src in (xxt, xyt):
+        def means(k):
+            mean_ps = ps_m.tile([P, 2, MEAN_N], F32, name="mean_ps")
+            for j in range(2):
+                i = 0
+                for nm in ("xx", "xy"):
                     for r in range(4):
                         nc.tensor.matmul(
-                            mean_ps[:, j, :],
-                            lhsT=src[:, j, P * r:P * r + P],
-                            rhs=negc[:],
-                            start=(k == 0),
-                            stop=(k == 7),
-                        )
-                        k += 1
-            negm = small.tile([P, 4], F32, name="negm")
-            nc.vector.tensor_copy(out=negm[:], in_=mean_ps[:, :, 0])
-            ssq = small.tile([P, 4], F32, name="ssq")
-            ats = []
-            for h in range(2):
-                a_sb = apool.tile([P, 2, NPOS], F32, name="a_sb")
-                nc.vector.tensor_tensor(
-                    out=a_sb[:], in0=xxt[:, 2 * h:2 * h + 2, :], in1=xyt[:, 2 * h:2 * h + 2, :], op=ALU.add
-                )
-                for i in range(2):
-                    at = ps_a.tile([P, NPOS], F32, name="at")
-                    for r in range(4):
-                        nc.tensor.transpose(at[:, P * r:P * r + P], a_sb[:, i, P * r:P * r + P], ident_f[:])
-                    ats.append(at)
-            for j in range(4):
-                junk = small.tile([P, NPOS], BF16, name="junk")
-                nc.scalar.activation(
-                    out=junk[:], in_=ats[j][:], func=ACT.Square,
-                    bias=negm[:, j:j + 1], scale=1.0, accum_out=ssq[:, j:j + 1],
-                )
-            state[(b, g)] = (ats, ssq)
+                            mean_ps[:, j, :], lhsT=st[(nm, k)][:, j, P * r:P * r + P], rhs=negc[:],
+                            start=(i == 0), stop=(i == 7))
+                        i += 1
+            st[("mean", k)] = mean_ps
 
-        gq = {}
-        gs = {}
+        def negmean(k):
+            negm = small.tile([P, 2], F32, name="negm")
+            nc.vector.tensor_copy(out=negm[:], in_=st[("mean", k)][:, :, 0])
+            st[("negm", k)] = negm
 
-        def back(b, g):
-            ats, ssq = state[(b, g)]
-            std = small.tile([P, 4], F32, name="std")
-            nc.scalar.activation(out=std[:], in_=ssq[:], func=ACT.Sqrt, scale=1.0 / (4.0 * (NPOS - 1)))
-            den = small.tile([P, 4], F32, name="den")
-            nc.vector.tensor_scalar(out=den[:], in0=std[:], scalar1=1e-8, scalar2=None, op0=ALU.add)
-            rec = small.tile([P, 4], F32, name="rec")
+        def add(k):
+            a_sb = apool.tile([P, 2, NPOS], F32, name="a_sb")
+            nc.vector.tensor_tensor(out=a_sb[:], in0=st[("xx", k)][:], in1=st[("xy", k)][:], op=ALU.add)
+            st[("a", k)] = a_sb
+
+        def tr(k, j):
+            at = ps_a.tile([P, NPOS], F32, name="at")
+            for r in range(4):
+                cols = slice(P * r, P * r + P)
+                if k in PE_ADD:
+                    nc.tensor.matmul(at[:, cols], lhsT=st[("xx", k)][:, j, cols], rhs=ident_b[:],
+                                     start=True, stop=False)
+                    nc.tensor.matmul(at[:, cols], lhsT=st[("xy", k)][:, j, cols], rhs=ident_b[:],
+                                     start=False, stop=True)
+                else:
+                    nc.tensor.transpose(at[:, cols], st[("a", k)][:, j, cols], ident_f[:])
+            st[("at", k, j)] = at
+
+        def sq(k, j):
+            if j == 0:
+                ssq_new = small.tile([P, 2], F32, name="ssq")
+                st[("ssq", k)] = ssq_new
+            junk = small.tile([P, NPOS], BF16, name="junk")
+            nc.scalar.activation(
+                out=junk[:], in_=st[("at", k, j)][:], func=ACT.Square,
+                bias=st[("negm", k)][:, j:j + 1], scale=1.0, accum_out=st[("ssq", k)][:, j:j + 1])
+
+        def root(k):
+            std = small.tile([P, 2], F32, name="std")
+            nc.scalar.activation(out=std[:], in_=st[("ssq", k)][:], func=ACT.Sqrt, scale=1.0 / (4.0 * (NPOS - 1)))
+            st[("std", k)] = std
+
+        def chain(k):
+            n0 = 2 * (k % 4)
+            den = small.tile([P, 2], F32, name="den")
+            nc.vector.tensor_scalar(out=den[:], in0=st[("std", k)][:], scalar1=1e-8, scalar2=None, op0=ALU.add)
+            rec = small.tile([P, 2], F32, name="rec")
             nc.vector.reciprocal(out=rec[:], in_=den[:])
-            sc = small.tile([P, 4], F32, name="sc")
-            nc.vector.tensor_tensor(out=sc[:], in0=rec[:], in1=w05[:, 4 * g:4 * g + 4], op=ALU.mult)
-            g_t = gpool.tile([P, 4, NPOS], BF16, name="g_t")
-            for j in range(4):
-                nc.scalar.activation(
-                    out=g_t[:, j, :].rearrange("c (p r) -> c p r", r=4),
-                    in_=ats[j][:].rearrange("c (r p) -> c p r", r=4),
-                    func=ACT.Copy, scale=sc[:, j:j + 1],
-                )
+            sc = small.tile([P, 2], F32, name="sc")
+            nc.vector.tensor_tensor(out=sc[:], in0=rec[:], in1=w05[:, n0:n0 + 2], op=ALU.mult)
+            st[("sc", k)] = sc
+
+        def ev(k, j):
+            u, t = k // 2, 2 * (k % 2) + j
+            if ("g_t", u) not in st:
+                g_new = gpool.tile([P, 4, NPOS], BF16, name="g_t")
+                st[("g_t", u)] = g_new
+            dst = st[("g_t", u)][:, t, :].rearrange("c (p r) -> c p r", r=4)
+            src = st[("at", k, j)][:].rearrange("c (r p) -> c p r", r=4)
+            if (k, j) in E_ON_V:
+                nc.vector.tensor_scalar(out=dst, in0=src, scalar1=st[("sc", k)][:, j:j + 1], scalar2=None,
+                                        op0=ALU.mult)
+            else:
+                nc.scalar.activation(out=dst, in_=src, func=ACT.Copy, scale=st[("sc", k)][:, j:j + 1])
+
+        def regroup(u):
             grp = gpool.tile([P, NPOS, 4], BF16, name="grp", align_bytes=64)
             nc.vector.tensor_copy(
                 out=grp[:].rearrange("p (c i) t -> p c t i", i=4),
-                in_=g_t[:].rearrange("p t (c i) -> p c t i", i=4),
-            )
-            codes = keep.tile([P, NPOS], U32, name="gq%d%d" % (b, g), align_bytes=64)
-            planes = keep.tile([P, NPOS], U8, name="gs%d%d" % (b, g), align_bytes=64)
+                in_=st[("g_t", u)][:].rearrange("p t (c i) -> p c t i", i=4))
+            st[("grp", u)] = grp
+
+        def quant(u):
+            codes = keep.tile([P, NPOS], U32, name="gq%d" % u, align_bytes=64)
+            planes = keep.tile([P, NPOS], U8, name="gs%d" % u, align_bytes=64)
             nc.vector.quantize_mx(
-                out=codes[:].bitcast(FP8X4), scales=planes[:], in_=grp[:].rearrange("p w t -> p (w t)")
-            )
-            gq[(b, g)] = codes
-            gs[(b, g)] = planes
+                out=codes[:].bitcast(FP8X4), scales=planes[:],
+                in_=st[("grp", u)][:].rearrange("p w t -> p (w t)"))
+            st[("gq", u)] = codes
+            st[("gs", u)] = planes
 
-        wq = []
-        ws = []
+        def wtr(m):
+            mc, i = m // 2, m % 2
+            wt = ps_w.tile([P, 2, 4, P], BF16, name="wt", tag="wacc")
+            for g in range(2):
+                for t in range(4):
+                    c0 = 512 * g + P * t
+                    nc.tensor.transpose(wt[:, g, t, :], st[("w", mc)][:, i, c0:c0 + P], ident_b[:])
+            st[("wt", m)] = wt
 
-        def wprep(mc):
-            wg = wpool.tile([P, 2, 2, P, 4], BF16, name="wg", align_bytes=64)
-            for i in range(2):
-                wt = ps_w.tile([P, 2, 4, P], BF16, name="wt", tag="wacc")
-                for g in range(2):
-                    for t in range(4):
-                        c0 = 512 * g + P * t
-                        nc.tensor.transpose(wt[:, g, t, :], w_sb[mc][:, i, c0:c0 + P], ident_b[:])
-                src = wt[:].rearrange("p g t o -> p g o t")
-                if i == 0:
-                    nc.vector.tensor_copy(out=wg[:, i], in_=src)
-                else:
-                    nc.scalar.copy(out=wg[:, i], in_=src)
+        def wev(m):
+            mc, i = m // 2, m % 2
+            if ("wg", mc) not in st:
+                wg_new = wpool.tile([P, 2, 2, P, 4], BF16, name="wg", align_bytes=64)
+                st[("wg", mc)] = wg_new
+            src = st[("wt", m)][:].rearrange("p g t o -> p g o t")
+            if m in W_ON_V:
+                nc.vector.tensor_copy(out=st[("wg", mc)][:, i], in_=src)
+            else:
+                nc.scalar.copy(out=st[("wg", mc)][:, i], in_=src)
+
+        def wquant(mc):
             codes = keep.tile([P, 4, P], U32, name="wq%d" % mc, align_bytes=64)
             planes = keep.tile([P, 4, P], U8, name="ws%d" % mc, align_bytes=64)
             nc.vector.quantize_mx(
                 out=codes[:].rearrange("p a o -> p (a o)").bitcast(FP8X4),
                 scales=planes[:].rearrange("p a o -> p (a o)"),
-                in_=wg[:].rearrange("p i g o t -> p (i g o t)"),
-            )
-            wq.append(codes)
-            ws.append(planes)
+                in_=st[("wg", mc)][:].rearrange("p i g o t -> p (i g o t)"))
+            st[("wq", mc)] = codes
+            st[("ws", mc)] = planes
 
-        xp = {}
+        def xprep(b, m):
+            mc, i = m // 2, m % 2
+            if ("xp", b, mc) not in st:
+                xp_new = keep.tile([P, 2, NPOS], F32, name="xp%d%d" % (b, mc))
+                st[("xp", b, mc)] = xp_new
+            dst = st[("xp", b, mc)][:, i, :]
+            if X_ENGINE[b] == "S":
+                nc.scalar.activation(out=dst, in_=st[("x", b)][:, m, :], func=ACT.Identity, bias=gb[:, m:m + 1], scale=1.0)
+            else:
+                eng = nc.gpsimd if X_ENGINE[b] == "G" else nc.vector
+                eng.tensor_scalar(out=dst, in0=st[("x", b)][:, m, :], scalar1=1.0, scalar2=gb[:, m:m + 1],
+                                  op0=ALU.mult, op1=ALU.add)
 
-        def xprep(b, mc):
-            t = keep.tile([P, 2, NPOS], F32, name="xp%d%d" % (b, mc))
-            for i in range(2):
-                m = 2 * mc + i
-                nc.gpsimd.tensor_scalar(
-                    out=t[:, i, :], in0=x_sb[b][:, m, :], scalar1=1.0, scalar2=gb[:, m:m + 1],
-                    op0=ALU.mult, op1=ALU.add,
-                )
-            xp[(b, mc)] = t
+        def mx(b, m):
+            mc, i = m // 2, m % 2
+            acc = ps_w.tile([P, NPOS], F32, name="acc", tag="wacc")
+            for n, g in enumerate((1, 0)):
+                nc.tensor.matmul_mx(
+                    out=acc[:],
+                    lhsT=st[("wq", mc)][:, 2 * i + g, :].bitcast(FP8X4),
+                    lhsT_scale=st[("ws", mc)][:, 2 * i + g, :],
+                    rhs=st[("gq", 2 * b + g)][:].bitcast(FP8X4),
+                    rhs_scale=st[("gs", 2 * b + g)][:],
+                    start=(n == 0), stop=(n == 1))
+            st[("acc", b, m)] = acc
 
-        def outp(b, mc):
-            t = xp[(b, mc)]
-            for i in range(2):
-                m = 2 * mc + i
-                acc = ps_w.tile([P, NPOS], F32, name="acc", tag="wacc")
-                for g in range(2):
-                    nc.tensor.matmul_mx(
-                        out=acc[:],
-                        lhsT=wq[mc][:, 2 * i + g, :].bitcast(FP8X4),
-                        lhsT_scale=ws[mc][:, 2 * i + g, :],
-                        rhs=gq[(b, g)][:].bitcast(FP8X4),
-                        rhs_scale=gs[(b, g)][:],
-                        start=(g == 0),
-                        stop=(g == 1),
-                    )
-                nc.vector.scalar_tensor_tensor(
-                    out=t[:, i, :], in0=acc[:], scalar=gam[:, m:m + 1], in1=t[:, i, :],
-                    op0=ALU.mult, op1=ALU.add,
-                )
+        def fin(b, m):
+            mc, i = m // 2, m % 2
+            t = st[("xp", b, mc)]
+            nc.vector.scalar_tensor_tensor(
+                out=t[:, i, :], in0=st[("acc", b, m)][:], scalar=gam[:, m:m + 1], in1=t[:, i, :],
+                op0=ALU.mult, op1=ALU.add)
+
+        def store(b, m0, n):
+            mc, i = m0 // 2, m0 % 2
             nc.sync.dma_start(
-                out=out[b].rearrange("(p m) h w -> p m (h w)", m=8)[:, 2 * mc:2 * mc + 2, :], in_=t[:]
-            )
+                out=out[b].rearrange("(p m) h w -> p m (h w)", m=8)[:, m0:m0 + n, :],
+                in_=st[("xp", b, mc)][:, i:i + n, :])
 
-        front(0, 0)
-        back(0, 0)
-        front(0, 1)
-        wprep(0)
-        back(0, 1)
-        wprep(1)
-        wprep(2)
-        wprep(3)
-        front(1, 0)
-        for mc in range(4):
-            xprep(0, mc)
-        outp(0, 0)
-        outp(0, 1)
-        back(1, 0)
-        front(1, 1)
-        outp(0, 2)
-        outp(0, 3)
-        for mc in range(4):
-            xprep(1, mc)
-        back(1, 1)
-        for mc in range(4):
-            outp(1, mc)
+        ops = {
+            "load_vec": load_vec, "load_a": load_a, "load_w": load_w, "load_x": load_x, "consts": consts,
+            "vec_w": vec_w, "vec_g": vec_g, "means": means, "negmean": negmean, "add": add, "tr": tr, "sq": sq,
+            "root": root, "chain": chain, "ev": ev, "regroup": regroup, "quant": quant, "wtr": wtr, "wev": wev,
+            "wquant": wquant, "xprep": xprep, "mx": mx, "fin": fin, "store": store,
+        }
+        for item in PLAN:
+            ops[item[0]](*item[1:])

@@ -14,447 +14,310 @@ ACT = mybir.ActivationFunctionType
 ALU = mybir.AluOpType
 
 P = 128
-NPOS = 512
-MEAN_N = 2
-PINNED = True
-PE_ADD = (0, 1, 4)
-W_ON_V = (1, 4, 7)
-E_ON_V = ()
-X_ENGINE = ('V', 'S')
-A_BUFS = 5
-AT_BUFS = 4
-WACC_BUFS = 3
-PLAN = (
-    ('load_vec',),
-    ('consts',),
-    ('load_a', 0, True),
-    ('load_a', 1, False),
-    ('load_a', 2, False),
-    ('load_a', 3, False),
-    ('load_w', 0),
-    ('load_w', 1),
-    ('load_a', 4, False),
-    ('load_w', 2),
-    ('load_a', 5, False),
-    ('load_w', 3),
-    ('load_a', 6, False),
-    ('load_x', 0),
-    ('load_a', 7, False),
-    ('load_x', 1),
-    ('tr', 0, 0),
-    ('means', 0),
-    ('negmean', 0),
-    ('tr', 0, 1),
-    ('means', 1),
-    ('sq', 0, 0),
-    ('negmean', 1),
-    ('tr', 1, 0),
-    ('vec_w',),
-    ('sq', 0, 1),
-    ('root', 0),
-    ('chain', 0),
-    ('sq', 1, 0),
-    ('tr', 1, 1),
-    ('sq', 1, 1),
-    ('means', 2),
-    ('root', 1),
-    ('add', 2),
-    ('negmean', 2),
-    ('means', 3),
-    ('ev', 0, 0),
-    ('tr', 2, 0),
-    ('chain', 1),
-    ('ev', 1, 0),
-    ('ev', 0, 1),
-    ('ev', 1, 1),
-    ('sq', 2, 0),
-    ('wtr', 1),
-    ('tr', 2, 1),
-    ('sq', 2, 1),
-    ('negmean', 3),
-    ('wtr', 0),
-    ('add', 3),
-    ('regroup', 0),
-    ('root', 2),
-    ('chain', 2),
-    ('means', 4),
-    ('quant', 0),
-    ('wev', 1),
-    ('wev', 0),
-    ('ev', 2, 0),
-    ('wtr', 3),
-    ('tr', 3, 0),
-    ('tr', 3, 1),
-    ('sq', 3, 0),
-    ('wtr', 4),
-    ('negmean', 4),
-    ('means', 5),
-    ('wev', 3),
-    ('ev', 2, 1),
-    ('sq', 3, 1),
-    ('wquant', 0),
-    ('vec_g',),
-    ('wev', 4),
-    ('tr', 4, 0),
-    ('sq', 4, 0),
-    ('negmean', 5),
-    ('wtr', 2),
-    ('root', 3),
-    ('add', 5),
-    ('chain', 3),
-    ('tr', 4, 1),
-    ('sq', 4, 1),
-    ('root', 4),
-    ('wtr', 7),
-    ('wev', 2),
-    ('add', 6),
-    ('wtr', 5),
-    ('means', 6),
-    ('negmean', 6),
-    ('chain', 4),
-    ('ev', 3, 0),
-    ('ev', 4, 0),
-    ('ev', 3, 1),
-    ('wquant', 1),
-    ('ev', 4, 1),
-    ('wev', 7),
-    ('tr', 6, 0),
-    ('sq', 6, 0),
-    ('tr', 5, 1),
-    ('xprep', 0, 1),
-    ('tr', 5, 0),
-    ('sq', 5, 0),
-    ('means', 7),
-    ('sq', 5, 1),
-    ('xprep', 0, 0),
-    ('root', 5),
-    ('wev', 5),
-    ('regroup', 1),
-    ('tr', 6, 1),
-    ('quant', 1),
-    ('mx', 0, 0),
-    ('xprep', 0, 3),
-    ('add', 7),
-    ('xprep', 0, 6),
-    ('sq', 6, 1),
-    ('fin', 0, 0),
-    ('wquant', 2),
-    ('root', 6),
-    ('wtr', 6),
-    ('mx', 0, 1),
-    ('wev', 6),
-    ('chain', 6),
-    ('xprep', 0, 4),
-    ('ev', 6, 0),
-    ('mx', 0, 2),
-    ('fin', 0, 1),
-    ('wquant', 3),
-    ('chain', 5),
-    ('ev', 6, 1),
-    ('mx', 0, 3),
-    ('fin', 0, 3),
-    ('negmean', 7),
-    ('ev', 5, 0),
-    ('xprep', 0, 2),
-    ('fin', 0, 2),
-    ('xprep', 0, 5),
-    ('ev', 5, 1),
-    ('regroup', 2),
-    ('tr', 7, 0),
-    ('sq', 7, 0),
-    ('mx', 0, 6),
-    ('tr', 7, 1),
-    ('sq', 7, 1),
-    ('root', 7),
-    ('quant', 2),
-    ('chain', 7),
-    ('mx', 0, 4),
-    ('ev', 7, 1),
-    ('mx', 0, 5),
-    ('fin', 0, 4),
-    ('store', 0, 2, 2),
-    ('fin', 0, 6),
-    ('mx', 0, 7),
-    ('fin', 0, 5),
-    ('ev', 7, 0),
-    ('regroup', 3),
-    ('quant', 3),
-    ('mx', 1, 0),
-    ('xprep', 1, 0),
-    ('xprep', 1, 1),
-    ('xprep', 0, 7),
-    ('xprep', 1, 5),
-    ('xprep', 1, 6),
-    ('fin', 0, 7),
-    ('xprep', 1, 4),
-    ('fin', 1, 0),
-    ('mx', 1, 1),
-    ('store', 0, 4, 2),
-    ('mx', 1, 2),
-    ('store', 0, 0, 2),
-    ('mx', 1, 3),
-    ('fin', 1, 1),
-    ('mx', 1, 4),
-    ('store', 0, 6, 2),
-    ('store', 1, 1, 1),
-    ('xprep', 1, 2),
-    ('fin', 1, 2),
-    ('store', 1, 0, 1),
-    ('xprep', 1, 3),
-    ('fin', 1, 3),
-    ('store', 1, 2, 2),
-    ('fin', 1, 4),
-    ('mx', 1, 5),
-    ('fin', 1, 5),
-    ('mx', 1, 6),
-    ('mx', 1, 7),
-    ('xprep', 1, 7),
-    ('fin', 1, 6),
-    ('store', 1, 4, 2),
-    ('fin', 1, 7),
-    ('store', 1, 6, 2),
-)
+POSITIONS = 512
+CHUNKS = 4
+PAIRS = 8
+ROW_TILES = 8
+MEAN_COLUMNS = 2
+ADDED_ON_TENSOR = (0, 1, 4)
 
 
 def tile_axialattentionblock_pb_kernel(tc, xx, xy, x, norm2_w, out_w, out_b, gamma_att, out):
     nc = tc.nc
     with ExitStack() as ctx:
         const = ctx.enter_context(tc.tile_pool(name="const", bufs=1))
-        inp = ctx.enter_context(tc.tile_pool(name="inp", bufs=1))
+        inputs = ctx.enter_context(tc.tile_pool(name="inputs", bufs=1))
         keep = ctx.enter_context(tc.tile_pool(name="keep", bufs=1))
-        apool = ctx.enter_context(tc.tile_pool(name="apool", bufs=A_BUFS))
-        gpool = ctx.enter_context(tc.tile_pool(name="gpool", bufs=2))
-        wpool = ctx.enter_context(tc.tile_pool(name="wpool", bufs=2))
+        sums = ctx.enter_context(tc.tile_pool(name="sums", bufs=4))
+        stage = ctx.enter_context(tc.tile_pool(name="stage", bufs=2))
         small = ctx.enter_context(tc.tile_pool(name="small", bufs=4))
-        ps_a = ctx.enter_context(tc.psum_pool(name="ps_a", bufs=AT_BUFS))
-        ps_m = ctx.enter_context(tc.psum_pool(name="ps_m", bufs=1))
-        ps_w = ctx.enter_context(tc.psum_pool(name="ps_w", bufs=WACC_BUFS))
-        if PINNED:
-            ctx.enter_context(tc.manual_schedule())
+        ps_heads = ctx.enter_context(tc.psum_pool(name="ps_heads", bufs=4))
+        ps_weights = ctx.enter_context(tc.psum_pool(name="ps_weights", bufs=2))
+        ps_products = ctx.enter_context(tc.psum_pool(name="ps_products", bufs=2))
+        ctx.enter_context(tc.manual_schedule())
 
         w_bf = const.tile([P, 8], BF16, name="w_bf")
-        gam_bf = const.tile([P, 8], BF16, name="gam_bf")
-        ob_bf = const.tile([P, 8], BF16, name="ob_bf")
-        one = const.tile([P, 1], F32, name="one")
-        warm = const.tile([P, 1], F32, name="warm")
-        negc = const.tile([P, MEAN_N], BF16, name="negc")
-        ident_f = const.tile([P, P], F32, name="ident_f")
-        ident_b = const.tile([P, P], BF16, name="ident_b")
-        gam = const.tile([P, 8], F32, name="gam")
-        gb = const.tile([P, 8], F32, name="gb")
-        w05 = const.tile([P, 8], F32, name="w05")
-        w_view = out_w.rearrange("(p m) j -> p m j", m=8)
-        st = {}
+        gamma_bf = const.tile([P, ROW_TILES], BF16, name="gamma_bf")
+        bias_bf = const.tile([P, ROW_TILES], BF16, name="bias_bf")
+        with nc.allow_non_contiguous_dma(reason="three vectors of 1,024 values, one or eight values to a piece"):
+            nc.scalar.dma_start(out=w_bf[:], in_=norm2_w.rearrange("(n c) -> c n", c=P))
+            nc.scalar.dma_start(out=gamma_bf[:], in_=gamma_att.rearrange("(p m) -> p m", m=ROW_TILES))
+            nc.scalar.dma_start(out=bias_bf[:], in_=out_b.rearrange("(p m) -> p m", m=ROW_TILES))
 
-        def load_vec():
-            with nc.allow_non_contiguous_dma(reason="three vectors of 1024 values"):
-                nc.scalar.dma_start(out=w_bf[:], in_=norm2_w.rearrange("(n c) -> c n", c=P))
-                nc.scalar.dma_start(out=gam_bf[:], in_=gamma_att.rearrange("(p m) -> p m", m=8))
-                nc.scalar.dma_start(out=ob_bf[:], in_=out_b.rearrange("(p m) -> p m", m=8))
+        xx_sb = []
+        xy_sb = []
+        w_sb = []
+        x_sb = []
 
-        def load_a(k, split):
+        def load_pair(k, by_head):
             b, n0 = k // 4, 2 * (k % 4)
             tiles = []
-            for nm in ("xx", "xy"):
-                t = inp.tile([P, 2, NPOS], BF16, name="%s_%d" % (nm, k))
-                st[(nm, k)] = t
+            for name, tiles_of in (("xx", xx_sb), ("xy", xy_sb)):
+                t = inputs.tile([P, 2, POSITIONS], BF16, name="%s_%d" % (name, k))
+                tiles_of.append(t)
                 tiles.append(t)
-            if split:
+            if by_head:
                 for j in range(2):
                     for src, t in zip((xx, xy), tiles):
                         nc.sync.dma_start(
-                            out=t[:, j, :], in_=src[b, n0 + j].rearrange("h (q r) c -> (h q) (r c)", r=4))
+                            out=t[:, j, :], in_=src[b, n0 + j].rearrange("h (q r) c -> (h q) (r c)", r=CHUNKS))
             else:
                 for src, t in zip((xx, xy), tiles):
                     nc.sync.dma_start(
-                        out=t[:], in_=src[b, n0:n0 + 2].rearrange("n h (q r) c -> (h q) n (r c)", r=4))
+                        out=t[:], in_=src[b, n0:n0 + 2].rearrange("n h (q r) c -> (h q) n (r c)", r=CHUNKS))
 
-        def load_w(mc):
-            t = inp.tile([P, 2, 1024], BF16, name="w_sb%d" % mc)
-            nc.sync.dma_start(out=t[:], in_=w_view[:, 2 * mc:2 * mc + 2, :])
-            st[("w", mc)] = t
+        def load_weights(i):
+            t = inputs.tile([P, 2, 1024], BF16, name="w_sb%d" % i)
+            nc.sync.dma_start(out=t[:], in_=out_w.rearrange("(p m) j -> p m j", m=ROW_TILES)[:, 2 * i:2 * i + 2, :])
+            w_sb.append(t)
 
-        def load_x(b):
-            t = inp.tile([P, 8, NPOS], BF16, name="x_sb%d" % b)
-            nc.sync.dma_start(out=t[:], in_=x[b].rearrange("(p m) h w -> p m (h w)", m=8))
-            st[("x", b)] = t
+        def load_residual(b):
+            t = inputs.tile([P, ROW_TILES, POSITIONS], BF16, name="x_sb%d" % b)
+            nc.sync.dma_start(out=t[:], in_=x[b].rearrange("(p m) h w -> p m (h w)", m=ROW_TILES))
+            x_sb.append(t)
 
-        def consts():
-            nc.vector.memset(one[:], 1.0)
-            nc.scalar.activation(out=warm[:], in_=one[:], func=ACT.Sqrt)
-            nc.vector.memset(negc[:], -1.0 / NPOS)
-            make_identity(nc, ident_b[:])
-            make_identity(nc, ident_f[:])
+        one = const.tile([P, 1], F32, name="one")
+        nc.vector.memset(one[:], 1.0)
+        warm = const.tile([P, 1], F32, name="warm")
+        nc.scalar.activation(out=warm[:], in_=one[:], func=ACT.Sqrt)
+        minus_mean_weight = const.tile([P, MEAN_COLUMNS], BF16, name="minus_mean_weight")
+        nc.vector.memset(minus_mean_weight[:], -1.0 / POSITIONS)
+        ident_bf = const.tile([P, P], BF16, name="ident_bf")
+        make_identity(nc, ident_bf[:])
+        ident_f32 = const.tile([P, P], F32, name="ident_f32")
+        make_identity(nc, ident_f32[:])
 
-        def vec_w():
-            nc.vector.tensor_scalar(out=w05[:], in0=w_bf[:], scalar1=0.5, scalar2=None, op0=ALU.mult)
+        load_pair(0, True)
+        for k in (1, 2, 3):
+            load_pair(k, False)
+        load_weights(0)
+        load_weights(1)
+        load_pair(4, False)
+        load_pair(5, False)
+        load_weights(2)
+        load_weights(3)
+        load_pair(6, False)
+        load_residual(0)
+        load_pair(7, False)
+        load_residual(1)
 
-        def vec_g():
-            nc.vector.tensor_copy(out=gam[:], in_=gam_bf[:])
-            nc.vector.tensor_tensor(out=gb[:], in0=gam_bf[:], in1=ob_bf[:], op=ALU.mult)
+        half_w = const.tile([P, 8], F32, name="half_w")
+        gamma = const.tile([P, ROW_TILES], F32, name="gamma")
+        gamma_bias = const.tile([P, ROW_TILES], F32, name="gamma_bias")
 
-        def means(k):
-            mean_ps = ps_m.tile([P, 2, MEAN_N], F32, name="mean_ps")
+        mean_ps = {}
+        minus_mean = {}
+        summed = {}
+        head_ps = {}
+        square_sum = {}
+        deviation = {}
+        factor = {}
+        scaled = {}
+        grouped = {}
+        g_codes = {}
+        g_scales = {}
+
+        def sum_positions(k):
+            t = ps_products.tile([P, 2, MEAN_COLUMNS], F32, name="mean_ps", tag="products")
             for j in range(2):
-                i = 0
-                for nm in ("xx", "xy"):
-                    for r in range(4):
-                        nc.tensor.matmul(
-                            mean_ps[:, j, :], lhsT=st[(nm, k)][:, j, P * r:P * r + P], rhs=negc[:],
-                            start=(i == 0), stop=(i == 7))
-                        i += 1
-            st[("mean", k)] = mean_ps
+                blocks = [src[k][:, j, P * r:P * r + P] for src in (xx_sb, xy_sb) for r in range(CHUNKS)]
+                for i, block in enumerate(blocks):
+                    nc.tensor.matmul(t[:, j, :], lhsT=block, rhs=minus_mean_weight[:],
+                                     start=(i == 0), stop=(i == len(blocks) - 1))
+            mean_ps[k] = t
 
-        def negmean(k):
-            negm = small.tile([P, 2], F32, name="negm")
-            nc.vector.tensor_copy(out=negm[:], in_=st[("mean", k)][:, :, 0])
-            st[("negm", k)] = negm
+        def fetch_mean_and_add(k):
+            t = small.tile([P, 2], F32, name="minus_mean")
+            nc.vector.tensor_copy(out=t[:], in_=mean_ps[k][:, :, 0])
+            minus_mean[k] = t
+            if k not in ADDED_ON_TENSOR:
+                s = sums.tile([P, 2, POSITIONS], F32, name="summed")
+                nc.vector.tensor_tensor(out=s[:], in0=xx_sb[k][:], in1=xy_sb[k][:], op=ALU.add)
+                summed[k] = s
 
-        def add(k):
-            a_sb = apool.tile([P, 2, NPOS], F32, name="a_sb")
-            nc.vector.tensor_tensor(out=a_sb[:], in0=st[("xx", k)][:], in1=st[("xy", k)][:], op=ALU.add)
-            st[("a", k)] = a_sb
-
-        def tr(k, j):
-            at = ps_a.tile([P, NPOS], F32, name="at")
-            for r in range(4):
+        def transpose_head(k, j):
+            t = ps_heads.tile([P, POSITIONS], F32, name="head_ps", tag="heads")
+            for r in range(CHUNKS):
                 cols = slice(P * r, P * r + P)
-                if k in PE_ADD:
-                    nc.tensor.matmul(at[:, cols], lhsT=st[("xx", k)][:, j, cols], rhs=ident_b[:],
-                                     start=True, stop=False)
-                    nc.tensor.matmul(at[:, cols], lhsT=st[("xy", k)][:, j, cols], rhs=ident_b[:],
-                                     start=False, stop=True)
+                if k in ADDED_ON_TENSOR:
+                    nc.tensor.matmul(t[:, cols], lhsT=xx_sb[k][:, j, cols], rhs=ident_bf[:], start=True, stop=False)
+                    nc.tensor.matmul(t[:, cols], lhsT=xy_sb[k][:, j, cols], rhs=ident_bf[:], start=False, stop=True)
                 else:
-                    nc.tensor.transpose(at[:, cols], st[("a", k)][:, j, cols], ident_f[:])
-            st[("at", k, j)] = at
+                    nc.tensor.transpose(t[:, cols], summed[k][:, j, cols], ident_f32[:])
+            head_ps[(k, j)] = t
 
-        def sq(k, j):
-            if j == 0:
-                ssq_new = small.tile([P, 2], F32, name="ssq")
-                st[("ssq", k)] = ssq_new
-            junk = small.tile([P, NPOS], BF16, name="junk")
-            nc.scalar.activation(
-                out=junk[:], in_=st[("at", k, j)][:], func=ACT.Square,
-                bias=st[("negm", k)][:, j:j + 1], scale=1.0, accum_out=st[("ssq", k)][:, j:j + 1])
+        def deviations(k):
+            sq = small.tile([P, 2], F32, name="square_sum")
+            for j in range(2):
+                unused = small.tile([P, POSITIONS], BF16, name="unused")
+                nc.scalar.activation(out=unused[:], in_=head_ps[(k, j)][:], func=ACT.Square,
+                                     bias=minus_mean[k][:, j:j + 1], scale=1.0, accum_out=sq[:, j:j + 1])
+            square_sum[k] = sq
+            d = small.tile([P, 2], F32, name="deviation")
+            nc.scalar.activation(out=d[:], in_=sq[:], func=ACT.Sqrt, scale=1.0 / (4.0 * (POSITIONS - 1)))
+            deviation[k] = d
 
-        def root(k):
-            std = small.tile([P, 2], F32, name="std")
-            nc.scalar.activation(out=std[:], in_=st[("ssq", k)][:], func=ACT.Sqrt, scale=1.0 / (4.0 * (NPOS - 1)))
-            st[("std", k)] = std
-
-        def chain(k):
+        def factors(k):
             n0 = 2 * (k % 4)
-            den = small.tile([P, 2], F32, name="den")
-            nc.vector.tensor_scalar(out=den[:], in0=st[("std", k)][:], scalar1=1e-8, scalar2=None, op0=ALU.add)
-            rec = small.tile([P, 2], F32, name="rec")
-            nc.vector.reciprocal(out=rec[:], in_=den[:])
-            sc = small.tile([P, 2], F32, name="sc")
-            nc.vector.tensor_tensor(out=sc[:], in0=rec[:], in1=w05[:, n0:n0 + 2], op=ALU.mult)
-            st[("sc", k)] = sc
+            denominator = small.tile([P, 2], F32, name="denominator")
+            nc.vector.tensor_scalar(out=denominator[:], in0=deviation[k][:], scalar1=1e-8, scalar2=None, op0=ALU.add)
+            inverse = small.tile([P, 2], F32, name="inverse")
+            nc.vector.reciprocal(out=inverse[:], in_=denominator[:])
+            f = small.tile([P, 2], F32, name="factor")
+            nc.vector.tensor_tensor(out=f[:], in0=inverse[:], in1=half_w[:, n0:n0 + 2], op=ALU.mult)
+            factor[k] = f
 
-        def ev(k, j):
+        def scale_head(k, j):
             u, t = k // 2, 2 * (k % 2) + j
-            if ("g_t", u) not in st:
-                g_new = gpool.tile([P, 4, NPOS], BF16, name="g_t")
-                st[("g_t", u)] = g_new
-            dst = st[("g_t", u)][:, t, :].rearrange("c (p r) -> c p r", r=4)
-            src = st[("at", k, j)][:].rearrange("c (r p) -> c p r", r=4)
-            if (k, j) in E_ON_V:
-                nc.vector.tensor_scalar(out=dst, in0=src, scalar1=st[("sc", k)][:, j:j + 1], scalar2=None,
-                                        op0=ALU.mult)
-            else:
-                nc.scalar.activation(out=dst, in_=src, func=ACT.Copy, scale=st[("sc", k)][:, j:j + 1])
+            if t == 0:
+                fresh = stage.tile([P, 4, POSITIONS], BF16, name="scaled")
+                scaled[u] = fresh
+            nc.scalar.activation(
+                out=scaled[u][:, t, :].rearrange("c (p r) -> c p r", r=CHUNKS),
+                in_=head_ps[(k, j)][:].rearrange("c (r p) -> c p r", r=CHUNKS),
+                func=ACT.Copy, scale=factor[k][:, j:j + 1])
 
         def regroup(u):
-            grp = gpool.tile([P, NPOS, 4], BF16, name="grp", align_bytes=64)
-            nc.vector.tensor_copy(
-                out=grp[:].rearrange("p (c i) t -> p c t i", i=4),
-                in_=st[("g_t", u)][:].rearrange("p t (c i) -> p c t i", i=4))
-            st[("grp", u)] = grp
+            t = stage.tile([P, POSITIONS, 4], BF16, name="grouped", align_bytes=64)
+            nc.vector.tensor_copy(out=t[:].rearrange("p (c i) t -> p c t i", i=4),
+                                  in_=scaled[u][:].rearrange("p t (c i) -> p c t i", i=4))
+            grouped[u] = t
 
-        def quant(u):
-            codes = keep.tile([P, NPOS], U32, name="gq%d" % u, align_bytes=64)
-            planes = keep.tile([P, NPOS], U8, name="gs%d" % u, align_bytes=64)
-            nc.vector.quantize_mx(
-                out=codes[:].bitcast(FP8X4), scales=planes[:],
-                in_=st[("grp", u)][:].rearrange("p w t -> p (w t)"))
-            st[("gq", u)] = codes
-            st[("gs", u)] = planes
+        def quantise_stream(u):
+            codes = keep.tile([P, POSITIONS], U32, name="g_codes%d" % u, align_bytes=64)
+            scales = keep.tile([P, POSITIONS], U8, name="g_scales%d" % u, align_bytes=64)
+            nc.vector.quantize_mx(out=codes[:].bitcast(FP8X4), scales=scales[:],
+                                  in_=grouped[u][:].rearrange("p w t -> p (w t)"))
+            g_codes[u] = codes
+            g_scales[u] = scales
 
-        def wtr(m):
-            mc, i = m // 2, m % 2
-            wt = ps_w.tile([P, 2, 4, P], BF16, name="wt", tag="wacc")
+        w_ps = {}
+        w_grouped = {}
+        w_codes = {}
+        w_scales = {}
+
+        def transpose_weights(m):
+            t = ps_weights.tile([P, 2, 4, P], BF16, name="w_ps")
             for g in range(2):
-                for t in range(4):
-                    c0 = 512 * g + P * t
-                    nc.tensor.transpose(wt[:, g, t, :], st[("w", mc)][:, i, c0:c0 + P], ident_b[:])
-            st[("wt", m)] = wt
+                for h in range(4):
+                    c0 = 512 * g + P * h
+                    nc.tensor.transpose(t[:, g, h, :], w_sb[m // 2][:, m % 2, c0:c0 + P], ident_bf[:])
+            w_ps[m] = t
 
-        def wev(m):
-            mc, i = m // 2, m % 2
-            if ("wg", mc) not in st:
-                wg_new = wpool.tile([P, 2, 2, P, 4], BF16, name="wg", align_bytes=64)
-                st[("wg", mc)] = wg_new
-            src = st[("wt", m)][:].rearrange("p g t o -> p g o t")
-            if m in W_ON_V:
-                nc.vector.tensor_copy(out=st[("wg", mc)][:, i], in_=src)
+        def copy_weights(m):
+            i = m % 2
+            if i == 0:
+                fresh = stage.tile([P, 2, 2, P, 4], BF16, name="w_grouped", align_bytes=64)
+                w_grouped[m // 2] = fresh
+            src = w_ps[m][:].rearrange("p g t o -> p g o t")
+            if i == 0:
+                nc.scalar.copy(out=w_grouped[m // 2][:, i], in_=src)
             else:
-                nc.scalar.copy(out=st[("wg", mc)][:, i], in_=src)
+                nc.vector.tensor_copy(out=w_grouped[m // 2][:, i], in_=src)
 
-        def wquant(mc):
-            codes = keep.tile([P, 4, P], U32, name="wq%d" % mc, align_bytes=64)
-            planes = keep.tile([P, 4, P], U8, name="ws%d" % mc, align_bytes=64)
-            nc.vector.quantize_mx(
-                out=codes[:].rearrange("p a o -> p (a o)").bitcast(FP8X4),
-                scales=planes[:].rearrange("p a o -> p (a o)"),
-                in_=st[("wg", mc)][:].rearrange("p i g o t -> p (i g o t)"))
-            st[("wq", mc)] = codes
-            st[("ws", mc)] = planes
+        def quantise_weights(i):
+            codes = keep.tile([P, 4, P], U32, name="w_codes%d" % i, align_bytes=64)
+            scales = keep.tile([P, 4, P], U8, name="w_scales%d" % i, align_bytes=64)
+            nc.vector.quantize_mx(out=codes[:].rearrange("p a o -> p (a o)").bitcast(FP8X4),
+                                  scales=scales[:].rearrange("p a o -> p (a o)"),
+                                  in_=w_grouped[i][:].rearrange("p i g o t -> p (i g o t)"))
+            w_codes[i] = codes
+            w_scales[i] = scales
 
-        def xprep(b, m):
-            mc, i = m // 2, m % 2
-            if ("xp", b, mc) not in st:
-                xp_new = keep.tile([P, 2, NPOS], F32, name="xp%d%d" % (b, mc))
-                st[("xp", b, mc)] = xp_new
-            dst = st[("xp", b, mc)][:, i, :]
-            if X_ENGINE[b] == "S":
-                nc.scalar.activation(out=dst, in_=st[("x", b)][:, m, :], func=ACT.Identity, bias=gb[:, m:m + 1], scale=1.0)
+        result = {}
+        product = {}
+
+        def residual(b, m):
+            if m % 2 == 0:
+                fresh = keep.tile([P, 2, POSITIONS], F32, name="result%d%d" % (b, m // 2))
+                result[(b, m // 2)] = fresh
+            dst = result[(b, m // 2)][:, m % 2, :]
+            if b == 0:
+                nc.vector.tensor_scalar(out=dst, in0=x_sb[b][:, m, :], scalar1=1.0, scalar2=gamma_bias[:, m:m + 1],
+                                        op0=ALU.mult, op1=ALU.add)
             else:
-                eng = nc.gpsimd if X_ENGINE[b] == "G" else nc.vector
-                eng.tensor_scalar(out=dst, in0=st[("x", b)][:, m, :], scalar1=1.0, scalar2=gb[:, m:m + 1],
-                                  op0=ALU.mult, op1=ALU.add)
+                nc.scalar.activation(out=dst, in_=x_sb[b][:, m, :], func=ACT.Identity,
+                                     bias=gamma_bias[:, m:m + 1], scale=1.0)
 
-        def mx(b, m):
-            mc, i = m // 2, m % 2
-            acc = ps_w.tile([P, NPOS], F32, name="acc", tag="wacc")
-            for n, g in enumerate((1, 0)):
+        def multiply(b, m):
+            if b == 0:
+                t = ps_products.tile([P, POSITIONS], F32, name="product", tag="products")
+            else:
+                t = ps_heads.tile([P, POSITIONS], F32, name="product", tag="heads")
+            for i, g in enumerate((1, 0)):
                 nc.tensor.matmul_mx(
-                    out=acc[:],
-                    lhsT=st[("wq", mc)][:, 2 * i + g, :].bitcast(FP8X4),
-                    lhsT_scale=st[("ws", mc)][:, 2 * i + g, :],
-                    rhs=st[("gq", 2 * b + g)][:].bitcast(FP8X4),
-                    rhs_scale=st[("gs", 2 * b + g)][:],
-                    start=(n == 0), stop=(n == 1))
-            st[("acc", b, m)] = acc
+                    out=t[:],
+                    lhsT=w_codes[m // 2][:, 2 * (m % 2) + g, :].bitcast(FP8X4),
+                    lhsT_scale=w_scales[m // 2][:, 2 * (m % 2) + g, :],
+                    rhs=g_codes[2 * b + g][:].bitcast(FP8X4),
+                    rhs_scale=g_scales[2 * b + g][:],
+                    start=(i == 0), stop=(i == 1))
+            product[(b, m)] = t
 
-        def fin(b, m):
-            mc, i = m // 2, m % 2
-            t = st[("xp", b, mc)]
-            nc.vector.scalar_tensor_tensor(
-                out=t[:, i, :], in0=st[("acc", b, m)][:], scalar=gam[:, m:m + 1], in1=t[:, i, :],
-                op0=ALU.mult, op1=ALU.add)
+        def finish(b, m):
+            t = result[(b, m // 2)]
+            nc.vector.scalar_tensor_tensor(out=t[:, m % 2, :], in0=product[(b, m)][:], scalar=gamma[:, m:m + 1],
+                                           in1=t[:, m % 2, :], op0=ALU.mult, op1=ALU.add)
+            if m % 2 == 1:
+                nc.sync.dma_start(
+                    out=out[b].rearrange("(p m) h w -> p m (h w)", m=ROW_TILES)[:, m - 1:m + 1, :], in_=t[:])
 
-        def store(b, m0, n):
-            mc, i = m0 // 2, m0 % 2
-            nc.sync.dma_start(
-                out=out[b].rearrange("(p m) h w -> p m (h w)", m=8)[:, m0:m0 + n, :],
-                in_=st[("xp", b, mc)][:, i:i + n, :])
+        nc.vector.tensor_scalar(out=half_w[:], in0=w_bf[:], scalar1=0.5, scalar2=None, op0=ALU.mult)
+        sum_positions(0)
+        fetch_mean_and_add(0)
+        transpose_head(0, 0)
+        transpose_head(0, 1)
+        sum_positions(1)
+        fetch_mean_and_add(1)
+        nc.vector.tensor_copy(out=gamma[:], in_=gamma_bf[:])
+        nc.vector.tensor_tensor(out=gamma_bias[:], in0=gamma_bf[:], in1=bias_bf[:], op=ALU.mult)
 
-        ops = {
-            "load_vec": load_vec, "load_a": load_a, "load_w": load_w, "load_x": load_x, "consts": consts,
-            "vec_w": vec_w, "vec_g": vec_g, "means": means, "negmean": negmean, "add": add, "tr": tr, "sq": sq,
-            "root": root, "chain": chain, "ev": ev, "regroup": regroup, "quant": quant, "wtr": wtr, "wev": wev,
-            "wquant": wquant, "xprep": xprep, "mx": mx, "fin": fin, "store": store,
-        }
-        for item in PLAN:
-            ops[item[0]](*item[1:])
+        for s in range(PAIRS + 1):
+            weights_now = (2 * s - 2, 2 * s - 1) if 1 <= s <= 4 else ()
+            outputs_now = (2 * s - 12, 2 * s - 11) if s >= 6 else ()
+            pass_now = (s - 3) // 2 if s >= 3 and s % 2 == 1 else None
+            if s + 2 < PAIRS:
+                sum_positions(s + 2)
+            for m in weights_now:
+                transpose_weights(m)
+            if s < PAIRS:
+                deviations(s)
+            if s + 2 < PAIRS:
+                fetch_mean_and_add(s + 2)
+            for j in range(2):
+                if s >= 1:
+                    scale_head(s - 1, j)
+                if s + 1 < PAIRS:
+                    transpose_head(s + 1, j)
+            for m in outputs_now:
+                multiply(0, m)
+            for m in weights_now:
+                copy_weights(m)
+            if s < PAIRS:
+                factors(s)
+            if pass_now is not None:
+                regroup(pass_now)
+            if weights_now:
+                quantise_weights(s - 1)
+            if pass_now is not None:
+                quantise_stream(pass_now)
+            if s == 5:
+                for m in range(ROW_TILES):
+                    residual(0, m)
+            for m in outputs_now:
+                finish(0, m)
+
+        regroup(3)
+        for m in range(ROW_TILES):
+            residual(1, m)
+        for m in (6, 7):
+            multiply(0, m)
+        quantise_stream(3)
+        for m in (6, 7):
+            finish(0, m)
+        for m in range(3):
+            multiply(1, m)
+        for m in range(ROW_TILES):
+            finish(1, m)
+            if m + 3 < ROW_TILES:
+                multiply(1, m + 3)

@@ -136,7 +136,10 @@ def tile_axialattentionblock_pb_kernel(tc, xx, xy, x, norm2_w, out_w, out_b, gam
                 summed[k] = s
 
         def transpose_head(k, j):
-            t = ps_heads.tile([P, POSITIONS], F32, name="head_ps", tag="heads")
+            if k == 6:
+                t = ps_weights.tile([P, POSITIONS], F32, name="head_ps", tag="w_ps")
+            else:
+                t = ps_heads.tile([P, POSITIONS], F32, name="head_ps", tag="heads")
             for r in range(CHUNKS):
                 cols = slice(P * r, P * r + P)
                 if k in ADDED_ON_TENSOR:
@@ -197,7 +200,7 @@ def tile_axialattentionblock_pb_kernel(tc, xx, xy, x, norm2_w, out_w, out_b, gam
         w_scales = {}
 
         def transpose_weights(m):
-            t = ps_weights.tile([P, 2, 4, P], BF16, name="w_ps")
+            t = ps_weights.tile([P, 2, 4, P], BF16, name="w_ps", tag="w_ps")
             for g in range(2):
                 for h in range(4):
                     c0 = 512 * g + P * h
@@ -258,9 +261,11 @@ def tile_axialattentionblock_pb_kernel(tc, xx, xy, x, norm2_w, out_w, out_b, gam
             t = result[(b, m // 2)]
             nc.vector.scalar_tensor_tensor(out=t[:, m % 2, :], in0=product[(b, m)][:], scalar=gamma[:, m:m + 1],
                                            in1=t[:, m % 2, :], op0=ALU.mult, op1=ALU.add)
-            if m % 2 == 1:
-                nc.sync.dma_start(
-                    out=out[b].rearrange("(p m) h w -> p m (h w)", m=ROW_TILES)[:, m - 1:m + 1, :], in_=t[:])
+            view = out[b].rearrange("(p m) h w -> p m (h w)", m=ROW_TILES)
+            if b == 1:
+                nc.sync.dma_start(out=view[:, m, :], in_=t[:, m % 2, :])
+            elif m % 2 == 1:
+                nc.sync.dma_start(out=view[:, m - 1:m + 1, :], in_=t[:])
 
         nc.vector.tensor_scalar(out=half_w[:], in0=w_bf[:], scalar1=0.5, scalar2=None, op0=ALU.mult)
         sum_positions(0)

@@ -36,11 +36,12 @@ def tile_axialattentionblock_pb_kernel(tc, xx, xy, x, norm2_w, out_w, out_b, gam
         ps_products = ctx.enter_context(tc.psum_pool(name="ps_products", bufs=2))
         ctx.enter_context(tc.manual_schedule())
 
-        w_bf = const.tile([P, 8], BF16, name="w_bf")
+        w_rows = const.tile([P, P], BF16, name="w_rows")
+        nc.vector.memset(w_rows[:], 0.0)
         gamma_bf = const.tile([P, ROW_TILES], BF16, name="gamma_bf")
         bias_bf = const.tile([P, ROW_TILES], BF16, name="bias_bf")
-        with nc.allow_non_contiguous_dma(reason="three vectors of 1,024 values, one or eight values to a piece"):
-            nc.scalar.dma_start(out=w_bf[:], in_=norm2_w.rearrange("(n c) -> c n", c=P))
+        nc.scalar.dma_start(out=w_rows[0:8, :], in_=norm2_w.rearrange("(n c) -> n c", c=P))
+        with nc.allow_non_contiguous_dma(reason="two vectors of 1,024 values, eight values to a partition"):
             nc.scalar.dma_start(out=gamma_bf[:], in_=gamma_att.rearrange("(p m) -> p m", m=ROW_TILES))
             nc.scalar.dma_start(out=bias_bf[:], in_=out_b.rearrange("(p m) -> p m", m=ROW_TILES))
 
@@ -267,13 +268,15 @@ def tile_axialattentionblock_pb_kernel(tc, xx, xy, x, norm2_w, out_w, out_b, gam
             elif m % 2 == 1:
                 nc.sync.dma_start(out=view[:, m - 1:m + 1, :], in_=t[:])
 
-        nc.vector.tensor_scalar(out=half_w[:], in0=w_bf[:], scalar1=0.5, scalar2=None, op0=ALU.mult)
         sum_positions(0)
         fetch_mean_and_add(0)
         transpose_head(0, 0)
         transpose_head(0, 1)
         sum_positions(1)
         fetch_mean_and_add(1)
+        w_columns = ps_weights.tile([P, P], BF16, name="w_columns", tag="w_ps")
+        nc.tensor.transpose(w_columns[:], w_rows[:], ident_bf[:])
+        nc.vector.tensor_scalar(out=half_w[:], in0=w_columns[:, 0:8], scalar1=0.5, scalar2=None, op0=ALU.mult)
         nc.vector.tensor_copy(out=gamma[:], in_=gamma_bf[:])
         nc.vector.tensor_tensor(out=gamma_bias[:], in0=gamma_bf[:], in1=bias_bf[:], op=ALU.mult)
 

@@ -41,9 +41,6 @@ def tile_axialattentionblock_pb_kernel(tc, xx, xy, x, norm2_w, out_w, out_b, gam
         gamma_bf = const.tile([P, ROW_TILES], BF16, name="gamma_bf")
         bias_bf = const.tile([P, ROW_TILES], BF16, name="bias_bf")
         nc.scalar.dma_start(out=w_rows[0:8, :], in_=norm2_w.rearrange("(n c) -> n c", c=P))
-        with nc.allow_non_contiguous_dma(reason="two vectors of 1,024 values, eight values to a partition"):
-            nc.scalar.dma_start(out=gamma_bf[:], in_=gamma_att.rearrange("(p m) -> p m", m=ROW_TILES))
-            nc.scalar.dma_start(out=bias_bf[:], in_=out_b.rearrange("(p m) -> p m", m=ROW_TILES))
 
         xx_sb = []
         xy_sb = []
@@ -92,11 +89,14 @@ def tile_axialattentionblock_pb_kernel(tc, xx, xy, x, norm2_w, out_w, out_b, gam
         for k in (1, 2, 3):
             load_pair(k, False)
         load_weights(0)
-        load_weights(1)
         load_pair(4, False)
+        load_weights(1)
         load_pair(5, False)
         load_weights(2)
         load_weights(3)
+        with nc.allow_non_contiguous_dma(reason="two vectors of 1,024 values, eight values to a partition"):
+            nc.sync.dma_start(out=gamma_bf[:], in_=gamma_att.rearrange("(p m) -> p m", m=ROW_TILES))
+            nc.sync.dma_start(out=bias_bf[:], in_=out_b.rearrange("(p m) -> p m", m=ROW_TILES))
         load_pair(6, False)
         load_residual(0)
         load_pair(7, False)
@@ -277,8 +277,6 @@ def tile_axialattentionblock_pb_kernel(tc, xx, xy, x, norm2_w, out_w, out_b, gam
         w_columns = ps_weights.tile([P, P], BF16, name="w_columns", tag="w_ps")
         nc.tensor.transpose(w_columns[:], w_rows[:], ident_bf[:])
         nc.vector.tensor_scalar(out=half_w[:], in0=w_columns[:, 0:8], scalar1=0.5, scalar2=None, op0=ALU.mult)
-        nc.vector.tensor_copy(out=gamma[:], in_=gamma_bf[:])
-        nc.vector.tensor_tensor(out=gamma_bias[:], in0=gamma_bf[:], in1=bias_bf[:], op=ALU.mult)
 
         for s in range(PAIRS + 1):
             weights_now = (2 * s - 2, 2 * s - 1) if 1 <= s <= 4 else ()
@@ -310,6 +308,8 @@ def tile_axialattentionblock_pb_kernel(tc, xx, xy, x, norm2_w, out_w, out_b, gam
             if pass_now is not None:
                 quantise_stream(pass_now)
             if s == 5:
+                nc.vector.tensor_copy(out=gamma[:], in_=gamma_bf[:])
+                nc.vector.tensor_tensor(out=gamma_bias[:], in0=gamma_bf[:], in1=bias_bf[:], op=ALU.mult)
                 for m in range(ROW_TILES):
                     residual(0, m)
             for m in outputs_now:

from contextlib import ExitStack

import concourse.mybir as mybir
from concourse.masks import make_identity

FLOPS = 2 * 1024 * 1024 * 1024

F32 = mybir.dt.float32
BF16 = mybir.dt.bfloat16
U32 = mybir.dt.uint32
U8 = mybir.dt.uint8
FP8X4 = mybir.dt.float8_e4m3fn_x4
ACT = mybir.ActivationFunctionType
ALU = mybir.AluOpType

P = 128
POSITIONS = 512
CHUNKS = 4
PAIRS = 8
ROW_TILES = 8
MEAN_COLUMNS = 2
ADDED_ON_TENSOR = (0, 1, 4)


def tile_axialattentionblock_pb_kernel(tc, xx, xy, x, norm2_w, out_w, out_b, gamma_att, out):
    nc = tc.nc
    with ExitStack() as ctx:
        const = ctx.enter_context(tc.tile_pool(name="const", bufs=1))
        inputs = ctx.enter_context(tc.tile_pool(name="inputs", bufs=1))
        keep = ctx.enter_context(tc.tile_pool(name="keep", bufs=1))
        sums = ctx.enter_context(tc.tile_pool(name="sums", bufs=4))
        stage = ctx.enter_context(tc.tile_pool(name="stage", bufs=2))
        small = ctx.enter_context(tc.tile_pool(name="small", bufs=4))
        ps_heads = ctx.enter_context(tc.psum_pool(name="ps_heads", bufs=4))
        ps_weights = ctx.enter_context(tc.psum_pool(name="ps_weights", bufs=2))
        ps_products = ctx.enter_context(tc.psum_pool(name="ps_products", bufs=2))
        ctx.enter_context(tc.manual_schedule())

        w_rows = const.tile([P, P], BF16, name="w_rows")
        nc.vector.memset(w_rows[:], 0.0)
        gamma_bf = const.tile([P, ROW_TILES], BF16, name="gamma_bf")
        bias_bf = const.tile([P, ROW_TILES], BF16, name="bias_bf")
        nc.scalar.dma_start(out=w_rows[0:8, :], in_=norm2_w.rearrange("(n c) -> n c", c=P))

        xx_sb = []
        xy_sb = []
        w_sb = []
        x_sb = []

        def load_pair(k, by_head):
            b, n0 = k // 4, 2 * (k % 4)
            tiles = []
            for name, tiles_of in (("xx", xx_sb), ("xy", xy_sb)):
                t = inputs.tile([P, 2, POSITIONS], BF16, name="%s_%d" % (name, k))
                tiles_of.append(t)
                tiles.append(t)
            if by_head:
                for j in range(2):
                    for src, t in zip((xx, xy), tiles):
                        nc.sync.dma_start(
                            out=t[:, j, :], in_=src[b, n0 + j].rearrange("h (q r) c -> (h q) (r c)", r=CHUNKS))
            else:
                for src, t in zip((xx, xy), tiles):
                    nc.sync.dma_start(
                        out=t[:], in_=src[b, n0:n0 + 2].rearrange("n h (q r) c -> (h q) n (r c)", r=CHUNKS))

        def load_weights(i):
            t = inputs.tile([P, 2, 1024], BF16, name="w_sb%d" % i)
            nc.sync.dma_start(out=t[:], in_=out_w.rearrange("(p m) j -> p m j", m=ROW_TILES)[:, 2 * i:2 * i + 2, :])
            w_sb.append(t)

        def load_residual(b):
            t = inputs.tile([P, ROW_TILES, POSITIONS], BF16, name="x_sb%d" % b)
            nc.sync.dma_start(out=t[:], in_=x[b].rearrange("(p m) h w -> p m (h w)", m=ROW_TILES))
            x_sb.append(t)

        one = const.tile([P, 1], F32, name="one")
        nc.vector.memset(one[:], 1.0)
        warm = const.tile([P, 1], F32, name="warm")
        nc.scalar.activation(out=warm[:], in_=one[:], func=ACT.Sqrt)
        minus_mean_weight = const.tile([P, MEAN_COLUMNS], BF16, name="minus_mean_weight")
        nc.vector.memset(minus_mean_weight[:], -1.0 / POSITIONS)
        ident_bf = const.tile([P, P], BF16, name="ident_bf")
        make_identity(nc, ident_bf[:])
        ident_f32 = const.tile([P, P], F32, name="ident_f32")
        make_identity(nc, ident_f32[:])

        load_pair(0, True)
        for k in (1, 2, 3):
            load_pair(k, False)
        load_weights(0)
        load_pair(4, False)
        load_weights(1)
        load_pair(5, False)
        load_weights(2)
        load_weights(3)
        with nc.allow_non_contiguous_dma(reason="two vectors of 1,024 values, eight values to a partition"):
            nc.sync.dma_start(out=gamma_bf[:], in_=gamma_att.rearrange("(p m) -> p m", m=ROW_TILES))
            nc.sync.dma_start(out=bias_bf[:], in_=out_b.rearrange("(p m) -> p m", m=ROW_TILES))
        load_pair(6, False)
        load_residual(0)
        load_pair(7, False)
        load_residual(1)

        half_w = const.tile([P, 8], F32, name="half_w")
        gamma = const.tile([P, ROW_TILES], F32, name="gamma")
        gamma_bias = const.tile([P, ROW_TILES], F32, name="gamma_bias")

        mean_ps = {}
        minus_mean = {}
        summed = {}
        head_ps = {}
        square_sum = {}
        deviation = {}
        factor = {}
        scaled = {}
        grouped = {}
        g_codes = {}
        g_scales = {}

        def sum_positions(k):
            t = ps_products.tile([P, 2, MEAN_COLUMNS], F32, name="mean_ps", tag="products")
            for j in range(2):
                blocks = [src[k][:, j, P * r:P * r + P] for src in (xx_sb, xy_sb) for r in range(CHUNKS)]
                for i, block in enumerate(blocks):
                    nc.tensor.matmul(t[:, j, :], lhsT=block, rhs=minus_mean_weight[:],
                                     start=(i == 0), stop=(i == len(blocks) - 1))
            mean_ps[k] = t

        def fetch_mean_and_add(k):
            t = small.tile([P, 2], F32, name="minus_mean")
            nc.vector.tensor_copy(out=t[:], in_=mean_ps[k][:, :, 0])
            minus_mean[k] = t
            if k not in ADDED_ON_TENSOR:
                s = sums.tile([P, 2, POSITIONS], F32, name="summed")
                nc.vector.tensor_tensor(out=s[:], in0=xx_sb[k][:], in1=xy_sb[k][:], op=ALU.add)
                summed[k] = s

        def transpose_head(k, j):
            if k == 6:
                t = ps_weights.tile([P, POSITIONS], F32, name="head_ps", tag="w_ps")
            else:
                t = ps_heads.tile([P, POSITIONS], F32, name="head_ps", tag="heads")
            for r in range(CHUNKS):
                cols = slice(P * r, P * r + P)
                if k in ADDED_ON_TENSOR:
                    nc.tensor.matmul(t[:, cols], lhsT=xx_sb[k][:, j, cols], rhs=ident_bf[:], start=True, stop=False)
                    nc.tensor.matmul(t[:, cols], lhsT=xy_sb[k][:, j, cols], rhs=ident_bf[:], start=False, stop=True)
                else:
                    nc.tensor.transpose(t[:, cols], summed[k][:, j, cols], ident_f32[:])
            head_ps[(k, j)] = t

        def deviations(k):
            sq = small.tile([P, 2], F32, name="square_sum")
            for j in range(2):
                unused = small.tile([P, POSITIONS], BF16, name="unused")
                nc.scalar.activation(out=unused[:], in_=head_ps[(k, j)][:], func=ACT.Square,
                                     bias=minus_mean[k][:, j:j + 1], scale=1.0, accum_out=sq[:, j:j + 1])
            square_sum[k] = sq
            d = small.tile([P, 2], F32, name="deviation")
            nc.scalar.activation(out=d[:], in_=sq[:], func=ACT.Sqrt, scale=1.0 / (4.0 * (POSITIONS - 1)))
            deviation[k] = d

        def factors(k):
            n0 = 2 * (k % 4)
            denominator = small.tile([P, 2], F32, name="denominator")
            nc.vector.tensor_scalar(out=denominator[:], in0=deviation[k][:], scalar1=1e-8, scalar2=None, op0=ALU.add)
            inverse = small.tile([P, 2], F32, name="inverse")
            nc.vector.reciprocal(out=inverse[:], in_=denominator[:])
            f = small.tile([P, 2], F32, name="factor")
            nc.vector.tensor_tensor(out=f[:], in0=inverse[:], in1=half_w[:, n0:n0 + 2], op=ALU.mult)
            factor[k] = f

        def scale_head(k, j):
            u, t = k // 2, 2 * (k % 2) + j
            if t == 0:
                fresh = stage.tile([P, 4, POSITIONS], BF16, name="scaled")
                scaled[u] = fresh
            nc.scalar.activation(
                out=scaled[u][:, t, :].rearrange("c (p r) -> c p r", r=CHUNKS),
                in_=head_ps[(k, j)][:].rearrange("c (r p) -> c p r", r=CHUNKS),
                func=ACT.Copy, scale=factor[k][:, j:j + 1])

        def regroup(u):
            t = stage.tile([P, POSITIONS, 4], BF16, name="grouped", align_bytes=64)
            nc.vector.tensor_copy(out=t[:].rearrange("p (c i) t -> p c t i", i=4),
                                  in_=scaled[u][:].rearrange("p t (c i) -> p c t i", i=4))
            grouped[u] = t

        def quantise_stream(u):
            codes = keep.tile([P, POSITIONS], U32, name="g_codes%d" % u, align_bytes=64)
            scales = keep.tile([P, POSITIONS], U8, name="g_scales%d" % u, align_bytes=64)
            nc.vector.quantize_mx(out=codes[:].bitcast(FP8X4), scales=scales[:],
                                  in_=grouped[u][:].rearrange("p w t -> p (w t)"))
            g_codes[u] = codes
            g_scales[u] = scales

        w_ps = {}
        w_grouped = {}
        w_codes = {}
        w_scales = {}

        def transpose_weights(m):
            t = ps_weights.tile([P, 2, 4, P], BF16, name="w_ps", tag="w_ps")
            for g in range(2):
                for h in range(4):
                    c0 = 512 * g + P * h
                    nc.tensor.transpose(t[:, g, h, :], w_sb[m // 2][:, m % 2, c0:c0 + P], ident_bf[:])
            w_ps[m] = t

        def copy_weights(m):
            i = m % 2
            if i == 0:
                fresh = stage.tile([P, 2, 2, P, 4], BF16, name="w_grouped", align_bytes=64)
                w_grouped[m // 2] = fresh
            src = w_ps[m][:].rearrange("p g t o -> p g o t")
            if i == 0:
                nc.scalar.copy(out=w_grouped[m // 2][:, i], in_=src)
            else:
                nc.vector.tensor_copy(out=w_grouped[m // 2][:, i], in_=src)

        def quantise_weights(i):
            codes = keep.tile([P, 4, P], U32, name="w_codes%d" % i, align_bytes=64)
            scales = keep.tile([P, 4, P], U8, name="w_scales%d" % i, align_bytes=64)
            nc.vector.quantize_mx(out=codes[:].rearrange("p a o -> p (a o)").bitcast(FP8X4),
                                  scales=scales[:].rearrange("p a o -> p (a o)"),
                                  in_=w_grouped[i][:].rearrange("p i g o t -> p (i g o t)"))
            w_codes[i] = codes
            w_scales[i] = scales

        result = {}
        product = {}

        def residual(b, m):
            if m % 2 == 0:
                fresh = keep.tile([P, 2, POSITIONS], F32, name="result%d%d" % (b, m // 2))
                result[(b, m // 2)] = fresh
            dst = result[(b, m // 2)][:, m % 2, :]
            if b == 0:
                nc.vector.tensor_scalar(out=dst, in0=x_sb[b][:, m, :], scalar1=1.0, scalar2=gamma_bias[:, m:m + 1],
                                        op0=ALU.mult, op1=ALU.add)
            else:
                nc.scalar.activation(out=dst, in_=x_sb[b][:, m, :], func=ACT.Identity,
                                     bias=gamma_bias[:, m:m + 1], scale=1.0)

        def multiply(b, m):
            if b == 0:
                t = ps_products.tile([P, POSITIONS], F32, name="product", tag="products")
            else:
                t = ps_heads.tile([P, POSITIONS], F32, name="product", tag="heads")
            for i, g in enumerate((1, 0)):
                nc.tensor.matmul_mx(
                    out=t[:],
                    lhsT=w_codes[m // 2][:, 2 * (m % 2) + g, :].bitcast(FP8X4),
                    lhsT_scale=w_scales[m // 2][:, 2 * (m % 2) + g, :],
                    rhs=g_codes[2 * b + g][:].bitcast(FP8X4),
                    rhs_scale=g_scales[2 * b + g][:],
                    start=(i == 0), stop=(i == 1))
            product[(b, m)] = t

        def finish(b, m):
            t = result[(b, m // 2)]
            nc.vector.scalar_tensor_tensor(out=t[:, m % 2, :], in0=product[(b, m)][:], scalar=gamma[:, m:m + 1],
                                           in1=t[:, m % 2, :], op0=ALU.mult, op1=ALU.add)
            view = out[b].rearrange("(p m) h w -> p m (h w)", m=ROW_TILES)
            if b == 1:
                nc.sync.dma_start(out=view[:, m, :], in_=t[:, m % 2, :])
            elif m % 2 == 1:
                nc.sync.dma_start(out=view[:, m - 1:m + 1, :], in_=t[:])

        sum_positions(0)
        fetch_mean_and_add(0)
        transpose_head(0, 0)
        transpose_head(0, 1)
        sum_positions(1)
        fetch_mean_and_add(1)
        w_columns = ps_weights.tile([P, P], BF16, name="w_columns", tag="w_ps")
        nc.tensor.transpose(w_columns[:], w_rows[:], ident_bf[:])
        nc.vector.tensor_scalar(out=half_w[:], in0=w_columns[:, 0:8], scalar1=0.5, scalar2=None, op0=ALU.mult)

        for s in range(PAIRS + 1):
            weights_now = (2 * s - 2, 2 * s - 1) if 1 <= s <= 4 else ()
            outputs_now = (2 * s - 12, 2 * s - 11) if s >= 6 else ()
            pass_now = (s - 3) // 2 if s >= 3 and s % 2 == 1 else None
            if s + 2 < PAIRS:
                sum_positions(s + 2)
            for m in weights_now:
                transpose_weights(m)
            if s < PAIRS:
                deviations(s)
            if s + 2 < PAIRS:
                fetch_mean_and_add(s + 2)
            for j in range(2):
                if s >= 1:
                    scale_head(s - 1, j)
                if s + 1 < PAIRS:
                    transpose_head(s + 1, j)
            for m in outputs_now:
                multiply(0, m)
            for m in weights_now:
                copy_weights(m)
            if s < PAIRS:
                factors(s)
            if pass_now is not None:
                regroup(pass_now)
            if weights_now:
                quantise_weights(s - 1)
            if pass_now is not None:
                quantise_stream(pass_now)
            if s == 5:
                nc.vector.tensor_copy(out=gamma[:], in_=gamma_bf[:])
                nc.vector.tensor_tensor(out=gamma_bias[:], in0=gamma_bf[:], in1=bias_bf[:], op=ALU.mult)
                for m in range(ROW_TILES):
                    residual(0, m)
            for m in outputs_now:
                finish(0, m)

        regroup(3)
        for m in range(ROW_TILES):
            residual(1, m)
        for m in (6, 7):
            multiply(0, m)
        quantise_stream(3)
        for m in (6, 7):
            finish(0, m)
        for m in range(3):
            multiply(1, m)
        for m in range(ROW_TILES):
            finish(1, m)
            if m + 3 < ROW_TILES:
                multiply(1, m + 3)
